import numpy as np
import ml_dtypes


def mxq(x, axis, fmt="e4m3"):
    dtype, down = {"e4m3": (ml_dtypes.float8_e4m3fn, 7), "e5m2": (ml_dtypes.float8_e5m2, 14)}[fmt]
    v = np.moveaxis(np.asarray(x, np.float32).astype(ml_dtypes.bfloat16).astype(np.float64), axis, -1)
    blocks = v.reshape(v.shape[:-1] + (-1, 32))
    amax = np.abs(blocks).max(-1, keepdims=True)
    byte = np.maximum(np.where(amax > 0, np.frexp(amax)[1] - 1 + 127, 0) - down, 1)
    scale = np.exp2(byte - 127.0)
    codes = (blocks / scale).astype(np.float32).astype(dtype).astype(np.float64)
    return np.moveaxis((codes * scale).reshape(v.shape), -1, axis)


WIDE = False


def mx_kscale(k):
    if not WIDE:
        return np.ones(k)
    levels = np.array([10, -10, 5, -5, 0])
    a = np.random.permutation(np.resize(levels, k // 512 * 4)).reshape(k // 512, 4)
    idx = np.arange(k)
    return np.exp2(a[idx // 512, idx % 128 // 32])


BF16 = ml_dtypes.bfloat16


def bf(x):
    return np.asarray(x, np.float32).astype(BF16)


def f64(x):
    return np.asarray(x).astype(np.float64)


B, A, S, R, H = 256, 32, 512, 512, 8192


def sigmoid(v):
    return 1.0 / (1.0 + np.exp(-v))


def elu(v):
    return np.where(v > 0.0, v, np.exp(np.minimum(v, 0.0)) - 1.0)


def setup_inputs():
    s = mx_kscale(H)
    return {"h": bf(elu(np.random.standard_normal((B, H))) * s),
            "prev_rnn_hidden": bf(np.random.standard_normal((B, R))),
            "W_ih": bf(np.random.standard_normal((3 * R, H)) / np.sqrt(H) / s[None, :]),
            "W_hh": bf(np.random.standard_normal((3 * R, R)) / np.sqrt(R)),
            "b_ih": bf(np.random.standard_normal(3 * R) * 0.3),
            "b_n": bf(np.random.standard_normal(R) * 0.3)}


def reference(h, prev_rnn_hidden, W_ih, W_hh, b_ih, b_n):
    hp = f64(prev_rnn_hidden)
    igates = (mxq(f64(h), 1, "e4m3") @ mxq(f64(W_ih), 1, "e4m3").T) + f64(b_ih)
    hgates = mxq(hp, 1, "e4m3") @ mxq(f64(W_hh), 1, "e4m3").T
    ig_r, ig_z, ig_n = np.split(igates, 3, axis=-1)
    hg_r, hg_z, hg_n = np.split(hgates, 3, axis=-1)
    reset = sigmoid(ig_r + hg_r)
    update = sigmoid(ig_z + hg_z)
    new = np.tanh(ig_n + reset * (hg_n + f64(b_n)))
    return new + update * (hp - new)

@@ -1,0 +1,303 @@
+from contextlib import ExitStack
+
+import concourse.mybir as mybir
+from concourse.masks import make_identity
+
+F32 = mybir.dt.float32
+BF16 = mybir.dt.bfloat16
+U32 = mybir.dt.uint32
+U8 = mybir.dt.uint8
+FP8X4 = mybir.dt.float8_e4m3fn_x4
+ACT = mybir.ActivationFunctionType
+ALU = mybir.AluOpType
+
+P = 128
+BATCH = 256
+HIDDEN = 512
+K_IH = 8192
+K_PASS = 512
+PASSES = K_IH // K_PASS
+ROW_BLOCKS = 3 * HIDDEN // P
+BLOCKS_PER_GATE = HIDDEN // P
+BANK_WORDS = 512
+CHUNK = 4096
+H_CHUNKS = BATCH * K_IH // (P * CHUNK)
+W_CHUNKS = 3 * HIDDEN * K_IH // (P * CHUNK)
+STREAM_BUFS = 8
+
+FLOPS = 2 * BATCH * 3 * HIDDEN * (K_IH + HIDDEN)
+
+
+def tile_prior_pa_k_kernel(tc, h, prev_rnn_hidden, W_ih, W_hh, b_ih, b_n, out):
+    nc = tc.nc
+    with ExitStack() as stack:
+        keep = stack.enter_context(tc.tile_pool(name="keep", bufs=1))
+        stream = stack.enter_context(tc.tile_pool(name="stream", bufs=STREAM_BUFS))
+        group_pool = stack.enter_context(tc.tile_pool(name="group", bufs=6))
+        code_pool = stack.enter_context(tc.tile_pool(name="code", bufs=6))
+        work = stack.enter_context(tc.tile_pool(name="work", bufs=2))
+        bank_pool = stack.enter_context(tc.psum_pool(name="bank", bufs=6))
+        acc_pool = stack.enter_context(tc.psum_pool(name="acc", bufs=2))
+        stack.enter_context(tc.manual_schedule())
+
+        ident_f32 = keep.tile([P, P], F32)
+        make_identity(nc, ident_f32[:])
+        ident_bf16 = keep.tile([P, P], BF16)
+        make_identity(nc, ident_bf16[:])
+        table_in = keep.tile([P, 1], F32)
+        table_out = keep.tile([P, 1], F32)
+        nc.vector.memset(table_in[:], 0.0)
+        nc.scalar.activation(out=table_out[:], in_=table_in[:], func=ACT.Sigmoid)
+        bias_rows = keep.tile([P, P], BF16)
+        nc.vector.memset(bias_rows[:], 0.0)
+
+        prev_sb = keep.tile([P, 2 * HIDDEN], BF16)
+        nc.sync.dma_start(
+            out=prev_sb[:].rearrange("p (t k) -> p t k", t=2),
+            in_=prev_rnn_hidden.rearrange("(t p) k -> p t k", p=P),
+        )
+        nc.scalar.dma_start(out=bias_rows[0:ROW_BLOCKS, :], in_=b_ih.rearrange("(j p) -> j p", p=P))
+        nc.scalar.dma_start(
+            out=bias_rows[ROW_BLOCKS : ROW_BLOCKS + BLOCKS_PER_GATE, :],
+            in_=b_n.rearrange("(j p) -> j p", p=P),
+        )
+        whh_sb = keep.tile([P, ROW_BLOCKS * HIDDEN], BF16)
+        nc.sync.dma_start(
+            out=whh_sb[:].rearrange("p (j k) -> p j k", j=ROW_BLOCKS),
+            in_=W_hh.rearrange("(j p) k -> p j k", p=P),
+        )
+
+        def load_chunk(i):
+            chunk = stream.tile([P, CHUNK], BF16)
+            if i < H_CHUNKS:
+                cols = CHUNK // 2
+                nc.sync.dma_start(
+                    out=chunk[:].rearrange("p (t k) -> p t k", t=2),
+                    in_=h.rearrange("(t p) k -> p t k", p=P)[:, :, cols * i : cols * (i + 1)],
+                )
+            else:
+                j, half = divmod(i - H_CHUNKS, 2)
+                nc.sync.dma_start(
+                    out=chunk[:],
+                    in_=W_ih[P * j : P * (j + 1), CHUNK * half : CHUNK * (half + 1)],
+                )
+            return chunk
+
+        chunks = {}
+        for i in range(STREAM_BUFS):
+            chunks[i] = load_chunk(i)
+
+        def transpose_and_group(blocks, slabs, vector_bank):
+            banks = len(blocks) // 4
+            grouped = group_pool.tile([P, 2 * BANK_WORDS * banks], BF16, align_bytes=64)
+            grouped_words = grouped[:].bitcast(F32)
+            for b in range(banks):
+                bank = bank_pool.tile([P, BANK_WORDS], F32, tag="bank")
+                for i in range(4):
+                    nc.tensor.transpose(bank[:, P * i : P * (i + 1)], blocks[4 * b + i], ident_f32[:])
+                src = bank[:].rearrange("p (s u c) -> p s c u", s=slabs, u=2)
+                dst = grouped_words[:, BANK_WORDS * b : BANK_WORDS * (b + 1)].rearrange(
+                    "p (s c u) -> p s c u", s=slabs, u=2
+                )
+                if b == vector_bank:
+                    nc.vector.tensor_copy(out=dst, in_=src)
+                else:
+                    nc.scalar.copy(out=dst, in_=src)
+            return grouped
+
+        def quantise(grouped, codes, scales):
+            nc.vector.quantize_mx(out=codes.bitcast(FP8X4), scales=scales, in_=grouped[:])
+
+        def mx_pass(acc, w_codes, w_scales, x_codes, x_scales, start, stop):
+            nc.tensor.matmul_mx(
+                out=acc,
+                lhsT=w_codes.bitcast(FP8X4),
+                lhsT_scale=w_scales,
+                rhs=x_codes.bitcast(FP8X4),
+                rhs_scale=x_scales,
+                start=start,
+                stop=stop,
+            )
+
+        prev_words = prev_sb[:].bitcast(F32)
+        prev_codes = keep.tile([P, BATCH], U32, align_bytes=64)
+        prev_scales = keep.tile([P, BATCH], U8, align_bytes=64)
+        prev_blocks = [
+            prev_words[:, 256 * t + P * u : 256 * t + P * (u + 1)] for u in range(2) for t in range(2)
+        ]
+        prev_grouped = transpose_and_group(prev_blocks, 1, 0)
+
+        prev_t_bank = bank_pool.tile([P, 2 * BANK_WORDS], BF16, tag="bank")
+        for f in range(BLOCKS_PER_GATE):
+            for t in range(2):
+                nc.tensor.transpose(
+                    prev_t_bank[:, BATCH * f + P * t : BATCH * f + P * (t + 1)],
+                    prev_sb[:, HIDDEN * t + P * f : HIDDEN * t + P * (f + 1)],
+                    ident_bf16[:],
+                )
+        prev_t = keep.tile([P, BLOCKS_PER_GATE * BATCH], F32)
+        nc.scalar.copy(out=prev_t[:], in_=prev_t_bank[:])
+
+        bias_bank = bank_pool.tile([P, 2 * BANK_WORDS], BF16, tag="bank")
+        nc.tensor.transpose(bias_bank[:, 0:P], bias_rows[:], ident_bf16[:])
+        bias_cols = keep.tile([P, ROW_BLOCKS + BLOCKS_PER_GATE], F32)
+        nc.vector.tensor_copy(out=bias_cols[:], in_=bias_bank[:, 0 : ROW_BLOCKS + BLOCKS_PER_GATE])
+        quantise(prev_grouped, prev_codes[:], prev_scales[:])
+
+        whh_words = whh_sb[:].bitcast(F32)
+        whh_codes = keep.tile([P, ROW_BLOCKS * P], U32, align_bytes=64)
+        whh_scales = keep.tile([P, ROW_BLOCKS * P], U8, align_bytes=64)
+        for piece in range(ROW_BLOCKS // 4):
+            blocks = [whh_words[:, P * i : P * (i + 1)] for i in range(8 * piece, 8 * piece + 8)]
+            grouped = transpose_and_group(blocks, 2, 1)
+            cols = slice(4 * P * piece, 4 * P * (piece + 1))
+            quantise(grouped, whh_codes[:, cols], whh_scales[:, cols])
+
+        def hh_pass(acc, j, start, stop):
+            cols = slice(P * j, P * (j + 1))
+            mx_pass(acc, whh_codes[:, cols], whh_scales[:, cols], prev_codes[:], prev_scales[:], start, stop)
+
+        h_codes = keep.tile([P, PASSES * BATCH], U32, align_bytes=64)
+        h_scales = keep.tile([P, PASSES * BATCH], U8, align_bytes=64)
+
+        def h_run(c):
+            words = chunks[c][:].bitcast(F32)
+            groups = []
+            for piece in range(2):
+                blocks = [
+                    words[:, 1024 * t + 256 * g + P * u : 1024 * t + 256 * g + P * (u + 1)]
+                    for g in (2 * piece, 2 * piece + 1)
+                    for u in range(2)
+                    for t in range(2)
+                ]
+                groups.append(transpose_and_group(blocks, 1, 1 if piece == 0 else None))
+            return groups
+
+        def h_quantise(c, groups):
+            for piece in range(2):
+                first = (2 * c + piece) * 2 * BATCH
+                cols = slice(first, first + 2 * BATCH)
+                quantise(groups[piece], h_codes[:, cols], h_scales[:, cols])
+
+        for c in range(H_CHUNKS):
+            groups = h_run(c)
+            chunks[c + STREAM_BUFS] = load_chunk(c + STREAM_BUFS)
+            h_quantise(c, groups)
+
+        w_codes = {}
+        w_scales = {}
+        accs = {}
+
+        def w_run(u):
+            words = chunks[H_CHUNKS + u][:].bitcast(F32)
+            groups = []
+            for piece in range(2):
+                blocks = [words[:, P * i : P * (i + 1)] for i in range(8 * piece, 8 * piece + 8)]
+                groups.append(transpose_and_group(blocks, 2, 1 if piece == 0 else None))
+            return groups
+
+        def w_quantise(u, groups):
+            for piece in range(2):
+                codes = code_pool.tile([P, 4 * P], U32, align_bytes=64)
+                scales = code_pool.tile([P, 4 * P], U8, align_bytes=64)
+                quantise(groups[piece], codes[:], scales[:])
+                w_codes[2 * u + piece] = codes
+                w_scales[2 * u + piece] = scales
+
+        def w_passes(u):
+            j, half = divmod(u, 2)
+            sums_hh = j < 2 * BLOCKS_PER_GATE
+            if half == 0:
+                acc = acc_pool.tile([P, BATCH], F32)
+                accs[j] = acc
+                if sums_hh:
+                    hh_pass(acc[:], j, True, False)
+            for s in range(8):
+                g = 8 * half + s
+                cols = slice(P * (s % 4), P * (s % 4 + 1))
+                mx_pass(
+                    accs[j][:],
+                    w_codes[2 * u + s // 4][:, cols],
+                    w_scales[2 * u + s // 4][:, cols],
+                    h_codes[:, BATCH * g : BATCH * (g + 1)],
+                    h_scales[:, BATCH * g : BATCH * (g + 1)],
+                    g == 0 and not sums_hh,
+                    g == PASSES - 1,
+                )
+
+        hn_b = keep.tile([P, BLOCKS_PER_GATE * BATCH], F32)
+        reset_hn = keep.tile([P, BLOCKS_PER_GATE * BATCH], F32)
+        update_prev = keep.tile([P, BLOCKS_PER_GATE * BATCH], F32)
+        one_less_update = keep.tile([P, BLOCKS_PER_GATE * BATCH], F32)
+        results = {}
+
+        def hn_products():
+            for pair in range(BLOCKS_PER_GATE // 2):
+                hn_bank = bank_pool.tile([P, BANK_WORDS], F32, tag="bank")
+                for i in range(2):
+                    f = 2 * pair + i
+                    hh_pass(hn_bank[:, BATCH * i : BATCH * (i + 1)], 2 * BLOCKS_PER_GATE + f, True, True)
+                for i in range(2):
+                    f = 2 * pair + i
+                    nc.scalar.activation(
+                        out=hn_b[:, BATCH * f : BATCH * (f + 1)],
+                        in_=hn_bank[:, BATCH * i : BATCH * (i + 1)],
+                        func=ACT.Identity,
+                        bias=bias_cols[:, ROW_BLOCKS + f : ROW_BLOCKS + f + 1],
+                    )
+
+        def gate(j):
+            kind, f = divmod(j, BLOCKS_PER_GATE)
+            cols = slice(BATCH * f, BATCH * (f + 1))
+            bias = bias_cols[:, j : j + 1]
+            if kind == 0:
+                reset = work.tile([P, BATCH], F32)
+                nc.scalar.activation(out=reset[:], in_=accs[j][:], func=ACT.Sigmoid, bias=bias)
+                nc.vector.tensor_tensor(out=reset_hn[:, cols], in0=hn_b[:, cols], in1=reset[:], op=ALU.mult)
+            elif kind == 1:
+                update = work.tile([P, BATCH], F32)
+                nc.scalar.activation(out=update[:], in_=accs[j][:], func=ACT.Sigmoid, bias=bias)
+                nc.vector.tensor_tensor(out=update_prev[:, cols], in0=update[:], in1=prev_t[:, cols], op=ALU.mult)
+                nc.vector.tensor_scalar(
+                    out=one_less_update[:, cols], in0=update[:], scalar1=-1.0, scalar2=1.0, op0=ALU.mult, op1=ALU.add
+                )
+            else:
+                pre = work.tile([P, BATCH], F32)
+                nc.vector.tensor_tensor(out=pre[:], in0=accs[j][:], in1=reset_hn[:, cols], op=ALU.add)
+                new = work.tile([P, BATCH], F32)
+                nc.scalar.activation(out=new[:], in_=pre[:], func=ACT.Tanh, bias=bias)
+                kept = work.tile([P, BATCH], F32)
+                nc.vector.tensor_tensor(out=kept[:], in0=new[:], in1=one_less_update[:, cols], op=ALU.mult)
+                result = work.tile([P, BATCH], F32, bufs=BLOCKS_PER_GATE)
+                nc.vector.tensor_tensor(out=result[:], in0=kept[:], in1=update_prev[:, cols], op=ALU.add)
+                results[f] = result
+
+        def store_block(f):
+            back = bank_pool.tile([P, BANK_WORDS], F32, tag="bank")
+            for t in range(2):
+                nc.tensor.transpose(back[:, P * t : P * (t + 1)], results[f][:, P * t : P * (t + 1)], ident_f32[:])
+            out_sb = work.tile([P, BATCH], F32)
+            nc.scalar.copy(out=out_sb[:], in_=back[:, 0:BATCH])
+            nc.sync.dma_start(
+                out=out.rearrange("(t p) r -> p t r", p=P)[:, :, P * f : P * (f + 1)],
+                in_=out_sb[:].rearrange("p (t r) -> p t r", t=2),
+            )
+
+        first_n = 2 * BLOCKS_PER_GATE
+        for u in range(W_CHUNKS + 1):
+            if u < W_CHUNKS:
+                groups = w_run(u)
+                if u % 2 == 0 and u // 2 - 2 >= first_n:
+                    store_block(u // 2 - 2 - first_n)
+                nxt = H_CHUNKS + u + STREAM_BUFS
+                if nxt < H_CHUNKS + W_CHUNKS:
+                    chunks[nxt] = load_chunk(nxt)
+                w_quantise(u, groups)
+            if u == 1:
+                hn_products()
+            if u >= 1:
+                w_passes(u - 1)
+                if (u - 1) % 2 == 1:
+                    gate((u - 1) // 2)
+        store_block(BLOCKS_PER_GATE - 2)
+        store_block(BLOCKS_PER_GATE - 1)

@@ -20,10 +20,11 @@ PASSES = K_IH // K_PASS
 ROW_BLOCKS = 3 * HIDDEN // P
 BLOCKS_PER_GATE = HIDDEN // P
 BANK_WORDS = 512
-CHUNK = 4096
-H_CHUNKS = BATCH * K_IH // (P * CHUNK)
-W_CHUNKS = 3 * HIDDEN * K_IH // (P * CHUNK)
-STREAM_BUFS = 8
+QUARTERS = 4
+QUARTER = K_IH // QUARTERS
+QUARTER_PASSES = PASSES // QUARTERS
+RUNS = ROW_BLOCKS // 2 * QUARTERS
+RUNS_AHEAD = 8
 
 FLOPS = 2 * BATCH * 3 * HIDDEN * (K_IH + HIDDEN)
 
@@ -32,7 +33,8 @@ def tile_prior_pa_k_kernel(tc, h, prev_rnn_hidden, W_ih, W_hh, b_ih, b_n, out):
     nc = tc.nc
     with ExitStack() as stack:
         keep = stack.enter_context(tc.tile_pool(name="keep", bufs=1))
-        stream = stack.enter_context(tc.tile_pool(name="stream", bufs=STREAM_BUFS))
+        h_pool = stack.enter_context(tc.tile_pool(name="h", bufs=QUARTERS))
+        w_pool = stack.enter_context(tc.tile_pool(name="w", bufs=2 * RUNS_AHEAD))
         group_pool = stack.enter_context(tc.tile_pool(name="group", bufs=6))
         code_pool = stack.enter_context(tc.tile_pool(name="code", bufs=6))
         work = stack.enter_context(tc.tile_pool(name="work", bufs=2))
@@ -61,31 +63,34 @@ def tile_prior_pa_k_kernel(tc, h, prev_rnn_hidden, W_ih, W_hh, b_ih, b_n, out):
             out=bias_rows[ROW_BLOCKS : ROW_BLOCKS + BLOCKS_PER_GATE, :],
             in_=b_n.rearrange("(j p) -> j p", p=P),
         )
+        h_sb = {}
         whh_sb = keep.tile([P, ROW_BLOCKS * HIDDEN], BF16)
-        nc.sync.dma_start(
-            out=whh_sb[:].rearrange("p (j k) -> p j k", j=ROW_BLOCKS),
-            in_=W_hh.rearrange("(j p) k -> p j k", p=P),
-        )
+        w_sb = {}
 
-        def load_chunk(i):
-            chunk = stream.tile([P, CHUNK], BF16)
-            if i < H_CHUNKS:
-                cols = CHUNK // 2
-                nc.sync.dma_start(
-                    out=chunk[:].rearrange("p (t k) -> p t k", t=2),
-                    in_=h.rearrange("(t p) k -> p t k", p=P)[:, :, cols * i : cols * (i + 1)],
-                )
-            else:
-                j, half = divmod(i - H_CHUNKS, 2)
-                nc.sync.dma_start(
-                    out=chunk[:],
-                    in_=W_ih[P * j : P * (j + 1), CHUNK * half : CHUNK * (half + 1)],
-                )
-            return chunk
+        def load_h(c):
+            h_piece = h_pool.tile([P, 2 * QUARTER], BF16)
+            nc.sync.dma_start(
+                out=h_piece[:].rearrange("p (t k) -> p t k", t=2),
+                in_=h.rearrange("(t p) k -> p t k", p=P)[:, :, QUARTER * c : QUARTER * (c + 1)],
+            )
+            h_sb[c] = h_piece
 
-        chunks = {}
-        for i in range(STREAM_BUFS):
-            chunks[i] = load_chunk(i)
+        def load_w(run):
+            pair, c = divmod(run, QUARTERS)
+            for j in (2 * pair, 2 * pair + 1):
+                piece = w_pool.tile([P, QUARTER], BF16)
+                nc.sync.dma_start(out=piece[:], in_=W_ih[P * j : P * (j + 1), QUARTER * c : QUARTER * (c + 1)])
+                w_sb[(j, c)] = piece
+
+        for run in range(RUNS_AHEAD):
+            if run < QUARTERS:
+                load_h(run)
+            load_w(run)
+            if run == 0:
+                nc.sync.dma_start(
+                    out=whh_sb[:].rearrange("p (j k) -> p j k", j=ROW_BLOCKS),
+                    in_=W_hh.rearrange("(j p) k -> p j k", p=P),
+                )
 
         def transpose_and_group(blocks, slabs, vector_bank):
             banks = len(blocks) // 4
@@ -144,24 +149,31 @@ def tile_prior_pa_k_kernel(tc, h, prev_rnn_hidden, W_ih, W_hh, b_ih, b_n, out):
         nc.vector.tensor_copy(out=bias_cols[:], in_=bias_bank[:, 0 : ROW_BLOCKS + BLOCKS_PER_GATE])
         quantise(prev_grouped, prev_codes[:], prev_scales[:])
 
-        whh_words = whh_sb[:].bitcast(F32)
         whh_codes = keep.tile([P, ROW_BLOCKS * P], U32, align_bytes=64)
         whh_scales = keep.tile([P, ROW_BLOCKS * P], U8, align_bytes=64)
-        for piece in range(ROW_BLOCKS // 4):
-            blocks = [whh_words[:, P * i : P * (i + 1)] for i in range(8 * piece, 8 * piece + 8)]
-            grouped = transpose_and_group(blocks, 2, 1)
-            cols = slice(4 * P * piece, 4 * P * (piece + 1))
-            quantise(grouped, whh_codes[:, cols], whh_scales[:, cols])
+
+        def whh_transposes():
+            words = whh_sb[:].bitcast(F32)
+            groups = []
+            for piece in range(ROW_BLOCKS // 4):
+                blocks = [words[:, P * i : P * (i + 1)] for i in range(8 * piece, 8 * piece + 8)]
+                groups.append(transpose_and_group(blocks, 2, 1 if piece % 2 == 0 else None))
+            return groups
+
+        def whh_quantise(groups):
+            for piece in range(ROW_BLOCKS // 4):
+                cols = slice(4 * P * piece, 4 * P * (piece + 1))
+                quantise(groups[piece], whh_codes[:, cols], whh_scales[:, cols])
 
         def hh_pass(acc, j, start, stop):
             cols = slice(P * j, P * (j + 1))
             mx_pass(acc, whh_codes[:, cols], whh_scales[:, cols], prev_codes[:], prev_scales[:], start, stop)
 
-        h_codes = keep.tile([P, PASSES * BATCH], U32, align_bytes=64)
-        h_scales = keep.tile([P, PASSES * BATCH], U8, align_bytes=64)
+        h_codes = {}
+        h_scales = {}
 
-        def h_run(c):
-            words = chunks[c][:].bitcast(F32)
+        def h_transposes(c):
+            words = h_sb[c][:].bitcast(F32)
             groups = []
             for piece in range(2):
                 blocks = [
@@ -174,56 +186,56 @@ def tile_prior_pa_k_kernel(tc, h, prev_rnn_hidden, W_ih, W_hh, b_ih, b_n, out):
             return groups
 
         def h_quantise(c, groups):
+            codes = h_pool.tile([P, QUARTER_PASSES * BATCH], U32, align_bytes=64)
+            scales = h_pool.tile([P, QUARTER_PASSES * BATCH], U8, align_bytes=64)
             for piece in range(2):
-                first = (2 * c + piece) * 2 * BATCH
-                cols = slice(first, first + 2 * BATCH)
-                quantise(groups[piece], h_codes[:, cols], h_scales[:, cols])
-
-        for c in range(H_CHUNKS):
-            groups = h_run(c)
-            chunks[c + STREAM_BUFS] = load_chunk(c + STREAM_BUFS)
-            h_quantise(c, groups)
+                cols = slice(2 * BATCH * piece, 2 * BATCH * (piece + 1))
+                quantise(groups[piece], codes[:, cols], scales[:, cols])
+            h_codes[c] = codes
+            h_scales[c] = scales
 
         w_codes = {}
         w_scales = {}
         accs = {}
 
-        def w_run(u):
-            words = chunks[H_CHUNKS + u][:].bitcast(F32)
+        def w_transposes(run):
+            pair, c = divmod(run, QUARTERS)
             groups = []
-            for piece in range(2):
-                blocks = [words[:, P * i : P * (i + 1)] for i in range(8 * piece, 8 * piece + 8)]
-                groups.append(transpose_and_group(blocks, 2, 1 if piece == 0 else None))
+            for i in range(2):
+                words = w_sb[(2 * pair + i, c)][:].bitcast(F32)
+                blocks = [words[:, P * b : P * (b + 1)] for b in range(8)]
+                groups.append(transpose_and_group(blocks, 2, 1 if i == 0 else None))
             return groups
 
-        def w_quantise(u, groups):
-            for piece in range(2):
-                codes = code_pool.tile([P, 4 * P], U32, align_bytes=64)
-                scales = code_pool.tile([P, 4 * P], U8, align_bytes=64)
-                quantise(groups[piece], codes[:], scales[:])
-                w_codes[2 * u + piece] = codes
-                w_scales[2 * u + piece] = scales
+        def w_quantise(run, groups):
+            pair, c = divmod(run, QUARTERS)
+            for i in range(2):
+                codes = code_pool.tile([P, QUARTER_PASSES * P], U32, align_bytes=64)
+                scales = code_pool.tile([P, QUARTER_PASSES * P], U8, align_bytes=64)
+                quantise(groups[i], codes[:], scales[:])
+                w_codes[(2 * pair + i, c)] = codes
+                w_scales[(2 * pair + i, c)] = scales
 
-        def w_passes(u):
-            j, half = divmod(u, 2)
-            sums_hh = j < 2 * BLOCKS_PER_GATE
-            if half == 0:
-                acc = acc_pool.tile([P, BATCH], F32)
-                accs[j] = acc
-                if sums_hh:
-                    hh_pass(acc[:], j, True, False)
-            for s in range(8):
-                g = 8 * half + s
-                cols = slice(P * (s % 4), P * (s % 4 + 1))
-                mx_pass(
-                    accs[j][:],
-                    w_codes[2 * u + s // 4][:, cols],
-                    w_scales[2 * u + s // 4][:, cols],
-                    h_codes[:, BATCH * g : BATCH * (g + 1)],
-                    h_scales[:, BATCH * g : BATCH * (g + 1)],
-                    g == 0 and not sums_hh,
-                    g == PASSES - 1,
-                )
+        def w_passes(run):
+            pair, c = divmod(run, QUARTERS)
+            for j in (2 * pair, 2 * pair + 1):
+                sums_hh = j < 2 * BLOCKS_PER_GATE
+                if c == 0:
+                    acc = acc_pool.tile([P, BATCH], F32)
+                    accs[j] = acc
+                for s in range(QUARTER_PASSES):
+                    g = QUARTER_PASSES * c + s
+                    mx_pass(
+                        accs[j][:],
+                        w_codes[(j, c)][:, P * s : P * (s + 1)],
+                        w_scales[(j, c)][:, P * s : P * (s + 1)],
+                        h_codes[c][:, BATCH * s : BATCH * (s + 1)],
+                        h_scales[c][:, BATCH * s : BATCH * (s + 1)],
+                        g == 0,
+                        g == PASSES - 1 and not sums_hh,
+                    )
+                if c == QUARTERS - 1 and sums_hh:
+                    hh_pass(accs[j][:], j, False, True)
 
         hn_b = keep.tile([P, BLOCKS_PER_GATE * BATCH], F32)
         reset_hn = keep.tile([P, BLOCKS_PER_GATE * BATCH], F32)
@@ -232,13 +244,13 @@ def tile_prior_pa_k_kernel(tc, h, prev_rnn_hidden, W_ih, W_hh, b_ih, b_n, out):
         results = {}
 
         def hn_products():
-            for pair in range(BLOCKS_PER_GATE // 2):
+            for half in range(BLOCKS_PER_GATE // 2):
                 hn_bank = bank_pool.tile([P, BANK_WORDS], F32, tag="bank")
                 for i in range(2):
-                    f = 2 * pair + i
+                    f = 2 * half + i
                     hh_pass(hn_bank[:, BATCH * i : BATCH * (i + 1)], 2 * BLOCKS_PER_GATE + f, True, True)
                 for i in range(2):
-                    f = 2 * pair + i
+                    f = 2 * half + i
                     nc.scalar.activation(
                         out=hn_b[:, BATCH * f : BATCH * (f + 1)],
                         in_=hn_bank[:, BATCH * i : BATCH * (i + 1)],
@@ -246,31 +258,51 @@ def tile_prior_pa_k_kernel(tc, h, prev_rnn_hidden, W_ih, W_hh, b_ih, b_n, out):
                         bias=bias_cols[:, ROW_BLOCKS + f : ROW_BLOCKS + f + 1],
                     )
 
-        def gate(j):
-            kind, f = divmod(j, BLOCKS_PER_GATE)
-            cols = slice(BATCH * f, BATCH * (f + 1))
-            bias = bias_cols[:, j : j + 1]
+        def gate_columns(j):
+            f = j % BLOCKS_PER_GATE
+            return slice(BATCH * f, BATCH * (f + 1))
+
+        def sigmoid_of(j):
+            gate = work.tile([P, BATCH], F32)
+            nc.scalar.activation(out=gate[:], in_=accs[j][:], func=ACT.Sigmoid, bias=bias_cols[:, j : j + 1])
+            return gate
+
+        def gates(pair):
+            blocks = (2 * pair, 2 * pair + 1)
+            kind = blocks[0] // BLOCKS_PER_GATE
             if kind == 0:
-                reset = work.tile([P, BATCH], F32)
-                nc.scalar.activation(out=reset[:], in_=accs[j][:], func=ACT.Sigmoid, bias=bias)
-                nc.vector.tensor_tensor(out=reset_hn[:, cols], in0=hn_b[:, cols], in1=reset[:], op=ALU.mult)
+                resets = [sigmoid_of(j) for j in blocks]
+                for i in range(2):
+                    cols = gate_columns(blocks[i])
+                    nc.vector.tensor_tensor(out=reset_hn[:, cols], in0=hn_b[:, cols], in1=resets[i][:], op=ALU.mult)
             elif kind == 1:
-                update = work.tile([P, BATCH], F32)
-                nc.scalar.activation(out=update[:], in_=accs[j][:], func=ACT.Sigmoid, bias=bias)
-                nc.vector.tensor_tensor(out=update_prev[:, cols], in0=update[:], in1=prev_t[:, cols], op=ALU.mult)
-                nc.vector.tensor_scalar(
-                    out=one_less_update[:, cols], in0=update[:], scalar1=-1.0, scalar2=1.0, op0=ALU.mult, op1=ALU.add
-                )
+                updates = [sigmoid_of(j) for j in blocks]
+                for i in range(2):
+                    cols = gate_columns(blocks[i])
+                    nc.vector.tensor_tensor(out=update_prev[:, cols], in0=updates[i][:], in1=prev_t[:, cols], op=ALU.mult)
+                    nc.vector.tensor_scalar(
+                        out=one_less_update[:, cols],
+                        in0=updates[i][:],
+                        scalar1=-1.0,
+                        scalar2=1.0,
+                        op0=ALU.mult,
+                        op1=ALU.add,
+                    )
             else:
-                pre = work.tile([P, BATCH], F32)
-                nc.vector.tensor_tensor(out=pre[:], in0=accs[j][:], in1=reset_hn[:, cols], op=ALU.add)
-                new = work.tile([P, BATCH], F32)
-                nc.scalar.activation(out=new[:], in_=pre[:], func=ACT.Tanh, bias=bias)
-                kept = work.tile([P, BATCH], F32)
-                nc.vector.tensor_tensor(out=kept[:], in0=new[:], in1=one_less_update[:, cols], op=ALU.mult)
-                result = work.tile([P, BATCH], F32, bufs=BLOCKS_PER_GATE)
-                nc.vector.tensor_tensor(out=result[:], in0=kept[:], in1=update_prev[:, cols], op=ALU.add)
-                results[f] = result
+                news = []
+                for j in blocks:
+                    pre = work.tile([P, BATCH], F32)
+                    nc.vector.tensor_tensor(out=pre[:], in0=accs[j][:], in1=reset_hn[:, gate_columns(j)], op=ALU.add)
+                    new = work.tile([P, BATCH], F32)
+                    nc.scalar.activation(out=new[:], in_=pre[:], func=ACT.Tanh, bias=bias_cols[:, j : j + 1])
+                    news.append(new)
+                for i in range(2):
+                    cols = gate_columns(blocks[i])
+                    kept = work.tile([P, BATCH], F32)
+                    nc.vector.tensor_tensor(out=kept[:], in0=news[i][:], in1=one_less_update[:, cols], op=ALU.mult)
+                    result = work.tile([P, BATCH], F32, bufs=BLOCKS_PER_GATE)
+                    nc.vector.tensor_tensor(out=result[:], in0=kept[:], in1=update_prev[:, cols], op=ALU.add)
+                    results[blocks[i] % BLOCKS_PER_GATE] = result
 
         def store_block(f):
             back = bank_pool.tile([P, BANK_WORDS], F32, tag="bank")
@@ -283,21 +315,27 @@ def tile_prior_pa_k_kernel(tc, h, prev_rnn_hidden, W_ih, W_hh, b_ih, b_n, out):
                 in_=out_sb[:].rearrange("p (t r) -> p t r", t=2),
             )
 
-        first_n = 2 * BLOCKS_PER_GATE
-        for u in range(W_CHUNKS + 1):
-            if u < W_CHUNKS:
-                groups = w_run(u)
-                if u % 2 == 0 and u // 2 - 2 >= first_n:
-                    store_block(u // 2 - 2 - first_n)
-                nxt = H_CHUNKS + u + STREAM_BUFS
-                if nxt < H_CHUNKS + W_CHUNKS:
-                    chunks[nxt] = load_chunk(nxt)
-                w_quantise(u, groups)
-            if u == 1:
+        first_n_run = 2 * BLOCKS_PER_GATE // 2 * QUARTERS
+        for run in range(RUNS + 1):
+            if run < RUNS:
+                if run < QUARTERS:
+                    h_groups = h_transposes(run)
+                w_groups = w_transposes(run)
+                if run == first_n_run + QUARTERS + 2:
+                    store_block(0)
+                    store_block(1)
+                if run + RUNS_AHEAD < RUNS:
+                    load_w(run + RUNS_AHEAD)
+                if run < QUARTERS:
+                    h_quantise(run, h_groups)
+                w_quantise(run, w_groups)
+                if run == 0:
+                    whh_quantise(whh_transposes())
+            if run == 1:
                 hn_products()
-            if u >= 1:
-                w_passes(u - 1)
-                if (u - 1) % 2 == 1:
-                    gate((u - 1) // 2)
-        store_block(BLOCKS_PER_GATE - 2)
-        store_block(BLOCKS_PER_GATE - 1)
+            if run >= 1:
+                w_passes(run - 1)
+                if (run - 1) % QUARTERS == QUARTERS - 1:
+                    gates((run - 1) // QUARTERS)
+        store_block(2)
+        store_block(3)

@@ -23,8 +23,9 @@ BANK_WORDS = 512
 QUARTERS = 4
 QUARTER = K_IH // QUARTERS
 QUARTER_PASSES = PASSES // QUARTERS
-RUNS = ROW_BLOCKS // 2 * QUARTERS
-RUNS_AHEAD = 8
+STEPS = ROW_BLOCKS // 2 * QUARTERS
+STEPS_AHEAD = 8
+RUN_STEPS = 2
 
 FLOPS = 2 * BATCH * 3 * HIDDEN * (K_IH + HIDDEN)
 
@@ -34,9 +35,9 @@ def tile_prior_pa_k_kernel(tc, h, prev_rnn_hidden, W_ih, W_hh, b_ih, b_n, out):
     with ExitStack() as stack:
         keep = stack.enter_context(tc.tile_pool(name="keep", bufs=1))
         h_pool = stack.enter_context(tc.tile_pool(name="h", bufs=QUARTERS))
-        w_pool = stack.enter_context(tc.tile_pool(name="w", bufs=2 * RUNS_AHEAD))
+        w_pool = stack.enter_context(tc.tile_pool(name="w", bufs=2 * STEPS_AHEAD))
         group_pool = stack.enter_context(tc.tile_pool(name="group", bufs=6))
-        code_pool = stack.enter_context(tc.tile_pool(name="code", bufs=6))
+        code_pool = stack.enter_context(tc.tile_pool(name="code", bufs=4 * RUN_STEPS + 2))
         work = stack.enter_context(tc.tile_pool(name="work", bufs=2))
         bank_pool = stack.enter_context(tc.psum_pool(name="bank", bufs=6))
         acc_pool = stack.enter_context(tc.psum_pool(name="acc", bufs=2))
@@ -75,18 +76,18 @@ def tile_prior_pa_k_kernel(tc, h, prev_rnn_hidden, W_ih, W_hh, b_ih, b_n, out):
             )
             h_sb[c] = h_piece
 
-        def load_w(run):
-            pair, c = divmod(run, QUARTERS)
+        def load_w(step):
+            pair, c = divmod(step, QUARTERS)
             for j in (2 * pair, 2 * pair + 1):
                 piece = w_pool.tile([P, QUARTER], BF16)
                 nc.sync.dma_start(out=piece[:], in_=W_ih[P * j : P * (j + 1), QUARTER * c : QUARTER * (c + 1)])
                 w_sb[(j, c)] = piece
 
-        for run in range(RUNS_AHEAD):
-            if run < QUARTERS:
-                load_h(run)
-            load_w(run)
-            if run == 0:
+        for step in range(STEPS_AHEAD):
+            if step < QUARTERS:
+                load_h(step)
+            load_w(step)
+            if step == 0:
                 nc.sync.dma_start(
                     out=whh_sb[:].rearrange("p (j k) -> p j k", j=ROW_BLOCKS),
                     in_=W_hh.rearrange("(j p) k -> p j k", p=P),
@@ -198,8 +199,8 @@ def tile_prior_pa_k_kernel(tc, h, prev_rnn_hidden, W_ih, W_hh, b_ih, b_n, out):
         w_scales = {}
         accs = {}
 
-        def w_transposes(run):
-            pair, c = divmod(run, QUARTERS)
+        def w_transposes(step):
+            pair, c = divmod(step, QUARTERS)
             groups = []
             for i in range(2):
                 words = w_sb[(2 * pair + i, c)][:].bitcast(F32)
@@ -207,8 +208,8 @@ def tile_prior_pa_k_kernel(tc, h, prev_rnn_hidden, W_ih, W_hh, b_ih, b_n, out):
                 groups.append(transpose_and_group(blocks, 2, 1 if i == 0 else None))
             return groups
 
-        def w_quantise(run, groups):
-            pair, c = divmod(run, QUARTERS)
+        def w_quantise(step, groups):
+            pair, c = divmod(step, QUARTERS)
             for i in range(2):
                 codes = code_pool.tile([P, QUARTER_PASSES * P], U32, align_bytes=64)
                 scales = code_pool.tile([P, QUARTER_PASSES * P], U8, align_bytes=64)
@@ -216,8 +217,8 @@ def tile_prior_pa_k_kernel(tc, h, prev_rnn_hidden, W_ih, W_hh, b_ih, b_n, out):
                 w_codes[(2 * pair + i, c)] = codes
                 w_scales[(2 * pair + i, c)] = scales
 
-        def w_passes(run):
-            pair, c = divmod(run, QUARTERS)
+        def w_passes(step):
+            pair, c = divmod(step, QUARTERS)
             for j in (2 * pair, 2 * pair + 1):
                 sums_hh = j < 2 * BLOCKS_PER_GATE
                 if c == 0:
@@ -315,27 +316,30 @@ def tile_prior_pa_k_kernel(tc, h, prev_rnn_hidden, W_ih, W_hh, b_ih, b_n, out):
                 in_=out_sb[:].rearrange("p (t r) -> p t r", t=2),
             )
 
-        first_n_run = 2 * BLOCKS_PER_GATE // 2 * QUARTERS
-        for run in range(RUNS + 1):
-            if run < RUNS:
-                if run < QUARTERS:
-                    h_groups = h_transposes(run)
-                w_groups = w_transposes(run)
-                if run == first_n_run + QUARTERS + 2:
-                    store_block(0)
-                    store_block(1)
-                if run + RUNS_AHEAD < RUNS:
-                    load_w(run + RUNS_AHEAD)
-                if run < QUARTERS:
-                    h_quantise(run, h_groups)
-                w_quantise(run, w_groups)
-                if run == 0:
-                    whh_quantise(whh_transposes())
-            if run == 1:
+        runs = [[step] for step in range(QUARTERS)]
+        runs += [list(range(step, step + RUN_STEPS)) for step in range(QUARTERS, STEPS, RUN_STEPS)]
+        for i in range(len(runs) + 1):
+            if i < len(runs):
+                for step in runs[i]:
+                    if step < QUARTERS:
+                        h_groups = h_transposes(step)
+                    w_groups = w_transposes(step)
+                    if step + STEPS_AHEAD < STEPS:
+                        load_w(step + STEPS_AHEAD)
+                    if step < QUARTERS:
+                        h_quantise(step, h_groups)
+                    w_quantise(step, w_groups)
+                    if step == 0:
+                        whh_quantise(whh_transposes())
+            if i == len(runs) - 1:
+                store_block(0)
+                store_block(1)
+            if i == 1:
                 hn_products()
-            if run >= 1:
-                w_passes(run - 1)
-                if (run - 1) % QUARTERS == QUARTERS - 1:
-                    gates((run - 1) // QUARTERS)
+            if i >= 1:
+                for step in runs[i - 1]:
+                    w_passes(step)
+                    if step % QUARTERS == QUARTERS - 1:
+                        gates(step // QUARTERS)
         store_block(2)
         store_block(3)

@@ -47,22 +47,22 @@ def tile_prior_pa_k_kernel(tc, h, prev_rnn_hidden, W_ih, W_hh, b_ih, b_n, out):
         make_identity(nc, ident_f32[:])
         ident_bf16 = keep.tile([P, P], BF16)
         make_identity(nc, ident_bf16[:])
+        bias_rows = keep.tile([P, P], BF16)
+        nc.vector.memset(bias_rows[:], 0.0)
+        nc.scalar.dma_start(out=bias_rows[0:ROW_BLOCKS, :], in_=b_ih.rearrange("(j p) -> j p", p=P))
+        nc.scalar.dma_start(
+            out=bias_rows[ROW_BLOCKS : ROW_BLOCKS + BLOCKS_PER_GATE, :],
+            in_=b_n.rearrange("(j p) -> j p", p=P),
+        )
         table_in = keep.tile([P, 1], F32)
         table_out = keep.tile([P, 1], F32)
         nc.vector.memset(table_in[:], 0.0)
         nc.scalar.activation(out=table_out[:], in_=table_in[:], func=ACT.Sigmoid)
-        bias_rows = keep.tile([P, P], BF16)
-        nc.vector.memset(bias_rows[:], 0.0)
 
         prev_sb = keep.tile([P, 2 * HIDDEN], BF16)
         nc.sync.dma_start(
             out=prev_sb[:].rearrange("p (t k) -> p t k", t=2),
             in_=prev_rnn_hidden.rearrange("(t p) k -> p t k", p=P),
-        )
-        nc.scalar.dma_start(out=bias_rows[0:ROW_BLOCKS, :], in_=b_ih.rearrange("(j p) -> j p", p=P))
-        nc.scalar.dma_start(
-            out=bias_rows[ROW_BLOCKS : ROW_BLOCKS + BLOCKS_PER_GATE, :],
-            in_=b_n.rearrange("(j p) -> j p", p=P),
         )
         h_sb = {}
         whh_sb = keep.tile([P, ROW_BLOCKS * HIDDEN], BF16)
@@ -144,11 +144,14 @@ def tile_prior_pa_k_kernel(tc, h, prev_rnn_hidden, W_ih, W_hh, b_ih, b_n, out):
         prev_t = keep.tile([P, BLOCKS_PER_GATE * BATCH], F32)
         nc.scalar.copy(out=prev_t[:], in_=prev_t_bank[:])
 
-        bias_bank = bank_pool.tile([P, 2 * BANK_WORDS], BF16, tag="bank")
-        nc.tensor.transpose(bias_bank[:, 0:P], bias_rows[:], ident_bf16[:])
-        bias_cols = keep.tile([P, ROW_BLOCKS + BLOCKS_PER_GATE], F32)
-        nc.vector.tensor_copy(out=bias_cols[:], in_=bias_bank[:, 0 : ROW_BLOCKS + BLOCKS_PER_GATE])
         quantise(prev_grouped, prev_codes[:], prev_scales[:])
+
+        bias_cols = keep.tile([P, ROW_BLOCKS + BLOCKS_PER_GATE], F32)
+
+        def bias_transpose():
+            bias_bank = bank_pool.tile([P, 2 * BANK_WORDS], BF16, tag="bank")
+            nc.tensor.transpose(bias_bank[:, 0:P], bias_rows[:], ident_bf16[:])
+            nc.vector.tensor_copy(out=bias_cols[:], in_=bias_bank[:, 0 : ROW_BLOCKS + BLOCKS_PER_GATE])
 
         whh_codes = keep.tile([P, ROW_BLOCKS * P], U32, align_bytes=64)
         whh_scales = keep.tile([P, ROW_BLOCKS * P], U8, align_bytes=64)
@@ -330,6 +333,7 @@ def tile_prior_pa_k_kernel(tc, h, prev_rnn_hidden, W_ih, W_hh, b_ih, b_n, out):
                         h_quantise(step, h_groups)
                     w_quantise(step, w_groups)
                     if step == 0:
+                        bias_transpose()
                         whh_quantise(whh_transposes())
             if i == len(runs) - 1:
                 store_block(0)

@@ -16,16 +16,20 @@ BATCH = 256
 HIDDEN = 512
 K_IH = 8192
 K_PASS = 512
-PASSES = K_IH // K_PASS
-ROW_BLOCKS = 3 * HIDDEN // P
-BLOCKS_PER_GATE = HIDDEN // P
+ROW_BLOCKS = 12
+GATE_BLOCKS = 4
 BANK_WORDS = 512
 QUARTERS = 4
 QUARTER = K_IH // QUARTERS
-QUARTER_PASSES = PASSES // QUARTERS
-STEPS = ROW_BLOCKS // 2 * QUARTERS
-STEPS_AHEAD = 8
-RUN_STEPS = 2
+QUARTER_PASSES = QUARTER // K_PASS
+RAW_BUFS = 24
+LPH = 1
+LPB = 1
+AHEAD = 16
+HEAD_BLOCKS = 2
+ACC_BANKS_HEAD = 2
+ACC_BANKS_LATER = 2
+LAG = 1
 
 FLOPS = 2 * BATCH * 3 * HIDDEN * (K_IH + HIDDEN)
 
@@ -34,14 +38,21 @@ def tile_prior_pa_k_kernel(tc, h, prev_rnn_hidden, W_ih, W_hh, b_ih, b_n, out):
     nc = tc.nc
     with ExitStack() as stack:
         keep = stack.enter_context(tc.tile_pool(name="keep", bufs=1))
-        h_pool = stack.enter_context(tc.tile_pool(name="h", bufs=QUARTERS))
-        w_pool = stack.enter_context(tc.tile_pool(name="w", bufs=2 * STEPS_AHEAD))
-        group_pool = stack.enter_context(tc.tile_pool(name="group", bufs=6))
-        code_pool = stack.enter_context(tc.tile_pool(name="code", bufs=4 * RUN_STEPS + 2))
+        raw_pool = stack.enter_context(tc.tile_pool(name="raw", bufs=RAW_BUFS))
+        group_pool = stack.enter_context(tc.tile_pool(name="group", bufs=8))
+        code_pool = stack.enter_context(tc.tile_pool(name="code", bufs=12))
         work = stack.enter_context(tc.tile_pool(name="work", bufs=2))
-        bank_pool = stack.enter_context(tc.psum_pool(name="bank", bufs=6))
-        acc_pool = stack.enter_context(tc.psum_pool(name="acc", bufs=2))
+        psum = stack.enter_context(tc.psum_pool(name="psum", bufs=1))
         stack.enter_context(tc.manual_schedule())
+
+        turn_banks = list(range(ACC_BANKS_HEAD, 8))
+        turn_next = [0]
+
+        def bank_tile(shape, dtype):
+            index = turn_banks[turn_next[0] % len(turn_banks)]
+            turn_next[0] += 1
+            bank = psum.tile(shape, dtype, tag="bank%d" % index)
+            return bank
 
         ident_f32 = keep.tile([P, P], F32)
         make_identity(nc, ident_f32[:])
@@ -51,64 +62,87 @@ def tile_prior_pa_k_kernel(tc, h, prev_rnn_hidden, W_ih, W_hh, b_ih, b_n, out):
         nc.vector.memset(bias_rows[:], 0.0)
         nc.scalar.dma_start(out=bias_rows[0:ROW_BLOCKS, :], in_=b_ih.rearrange("(j p) -> j p", p=P))
         nc.scalar.dma_start(
-            out=bias_rows[ROW_BLOCKS : ROW_BLOCKS + BLOCKS_PER_GATE, :],
-            in_=b_n.rearrange("(j p) -> j p", p=P),
+            out=bias_rows[ROW_BLOCKS : ROW_BLOCKS + GATE_BLOCKS, :], in_=b_n.rearrange("(j p) -> j p", p=P)
         )
         table_in = keep.tile([P, 1], F32)
         table_out = keep.tile([P, 1], F32)
         nc.vector.memset(table_in[:], 0.0)
         nc.scalar.activation(out=table_out[:], in_=table_in[:], func=ACT.Sigmoid)
 
+        block_order = [0, 1, 2, 3, 8, 9, 10, 11, 4, 5, 6, 7]
+
+        items = [("whh", piece, 0) for piece in range(3)]
+        head = block_order[:HEAD_BLOCKS]
+        for c0 in range(0, QUARTERS, LPH):
+            items += [("h", c, 0) for c in range(c0, c0 + LPH)]
+            for j in head:
+                items += [("w", j, c) for c in range(c0, c0 + LPH)]
+        for j in block_order[HEAD_BLOCKS:]:
+            items += [("w", j, c) for c in range(QUARTERS)]
+
+        raw = {}
         prev_sb = keep.tile([P, 2 * HIDDEN], BF16)
         nc.sync.dma_start(
             out=prev_sb[:].rearrange("p (t k) -> p t k", t=2),
             in_=prev_rnn_hidden.rearrange("(t p) k -> p t k", p=P),
         )
-        h_sb = {}
-        whh_sb = keep.tile([P, ROW_BLOCKS * HIDDEN], BF16)
-        w_sb = {}
 
-        def load_h(c):
-            h_piece = h_pool.tile([P, 2 * QUARTER], BF16)
-            nc.sync.dma_start(
-                out=h_piece[:].rearrange("p (t k) -> p t k", t=2),
-                in_=h.rearrange("(t p) k -> p t k", p=P)[:, :, QUARTER * c : QUARTER * (c + 1)],
-            )
-            h_sb[c] = h_piece
-
-        def load_w(step):
-            pair, c = divmod(step, QUARTERS)
-            for j in (2 * pair, 2 * pair + 1):
-                piece = w_pool.tile([P, QUARTER], BF16)
-                nc.sync.dma_start(out=piece[:], in_=W_ih[P * j : P * (j + 1), QUARTER * c : QUARTER * (c + 1)])
-                w_sb[(j, c)] = piece
-
-        for step in range(STEPS_AHEAD):
-            if step < QUARTERS:
-                load_h(step)
-            load_w(step)
-            if step == 0:
+        def load(item):
+            kind, a, c = item
+            if kind == "whh":
+                piece = raw_pool.tile([P, QUARTER], BF16, tag="raw1")
                 nc.sync.dma_start(
-                    out=whh_sb[:].rearrange("p (j k) -> p j k", j=ROW_BLOCKS),
-                    in_=W_hh.rearrange("(j p) k -> p j k", p=P),
+                    out=piece[:].rearrange("p (j k) -> p j k", j=4),
+                    in_=W_hh[4 * P * a : 4 * P * (a + 1), :].rearrange("(j p) k -> p j k", p=P),
                 )
+                raw[item] = [piece[:]]
+                return
+            lp = LPH if (kind == "h" or a in head) else LPB
+            q = a if kind == "h" else c
+            if q % lp != 0:
+                return
+            if kind == "h":
+                for cc in range(q, q + lp):
+                    raw[("h", cc, 0)] = []
+                for t in range(2):
+                    piece = raw_pool.tile([P, lp * QUARTER], BF16, tag="raw%d" % lp, bufs=RAW_BUFS // lp)
+                    nc.sync.dma_start(out=piece[:], in_=h[P * t : P * (t + 1), QUARTER * q : QUARTER * (q + lp)])
+                    for i in range(lp):
+                        raw[("h", q + i, 0)].append(piece[:, QUARTER * i : QUARTER * (i + 1)])
+            else:
+                piece = raw_pool.tile([P, lp * QUARTER], BF16, tag="raw%d" % lp, bufs=RAW_BUFS // lp)
+                nc.sync.dma_start(out=piece[:], in_=W_ih[P * a : P * (a + 1), QUARTER * q : QUARTER * (q + lp)])
+                for i in range(lp):
+                    raw[("w", a, q + i)] = [piece[:, QUARTER * i : QUARTER * (i + 1)]]
 
-        def transpose_and_group(blocks, slabs, vector_bank):
+        loaded = [0]
+
+        def load_ahead(upto):
+            for index in range(loaded[0], min(len(items), upto)):
+                load(items[index])
+                loaded[0] = index + 1
+
+        load_ahead(AHEAD)
+
+        banks_used = [0]
+
+        def transpose_and_group(blocks, slabs):
             banks = len(blocks) // 4
-            grouped = group_pool.tile([P, 2 * BANK_WORDS * banks], BF16, align_bytes=64)
+            grouped = group_pool.tile([P, 2 * BANK_WORDS * banks], BF16, align_bytes=64, tag="grouped")
             grouped_words = grouped[:].bitcast(F32)
             for b in range(banks):
-                bank = bank_pool.tile([P, BANK_WORDS], F32, tag="bank")
+                bank = bank_tile([P, BANK_WORDS], F32)
                 for i in range(4):
                     nc.tensor.transpose(bank[:, P * i : P * (i + 1)], blocks[4 * b + i], ident_f32[:])
                 src = bank[:].rearrange("p (s u c) -> p s c u", s=slabs, u=2)
                 dst = grouped_words[:, BANK_WORDS * b : BANK_WORDS * (b + 1)].rearrange(
                     "p (s c u) -> p s c u", s=slabs, u=2
                 )
-                if b == vector_bank:
+                if banks_used[0] % 4 == 1:
                     nc.vector.tensor_copy(out=dst, in_=src)
                 else:
                     nc.scalar.copy(out=dst, in_=src)
+                banks_used[0] += 1
             return grouped
 
         def quantise(grouped, codes, scales):
@@ -116,234 +150,188 @@ def tile_prior_pa_k_kernel(tc, h, prev_rnn_hidden, W_ih, W_hh, b_ih, b_n, out):
 
         def mx_pass(acc, w_codes, w_scales, x_codes, x_scales, start, stop):
             nc.tensor.matmul_mx(
-                out=acc,
-                lhsT=w_codes.bitcast(FP8X4),
-                lhsT_scale=w_scales,
-                rhs=x_codes.bitcast(FP8X4),
-                rhs_scale=x_scales,
-                start=start,
-                stop=stop,
+                out=acc, lhsT=w_codes.bitcast(FP8X4), lhsT_scale=w_scales,
+                rhs=x_codes.bitcast(FP8X4), rhs_scale=x_scales, start=start, stop=stop,
             )
 
         prev_words = prev_sb[:].bitcast(F32)
         prev_codes = keep.tile([P, BATCH], U32, align_bytes=64)
         prev_scales = keep.tile([P, BATCH], U8, align_bytes=64)
-        prev_blocks = [
-            prev_words[:, 256 * t + P * u : 256 * t + P * (u + 1)] for u in range(2) for t in range(2)
-        ]
-        prev_grouped = transpose_and_group(prev_blocks, 1, 0)
-
-        prev_t_bank = bank_pool.tile([P, 2 * BANK_WORDS], BF16, tag="bank")
-        for f in range(BLOCKS_PER_GATE):
-            for t in range(2):
-                nc.tensor.transpose(
-                    prev_t_bank[:, BATCH * f + P * t : BATCH * f + P * (t + 1)],
-                    prev_sb[:, HIDDEN * t + P * f : HIDDEN * t + P * (f + 1)],
-                    ident_bf16[:],
-                )
-        prev_t = keep.tile([P, BLOCKS_PER_GATE * BATCH], F32)
-        nc.scalar.copy(out=prev_t[:], in_=prev_t_bank[:])
-
-        quantise(prev_grouped, prev_codes[:], prev_scales[:])
-
-        bias_cols = keep.tile([P, ROW_BLOCKS + BLOCKS_PER_GATE], F32)
+        prev_blocks = [prev_words[:, 256 * t + P * u : 256 * t + P * (u + 1)] for u in range(2) for t in range(2)]
+        prev_grouped = transpose_and_group(prev_blocks, 1)
+        bias_cols = keep.tile([P, ROW_BLOCKS + GATE_BLOCKS], F32)
+        bias_neg = keep.tile([P, ROW_BLOCKS + GATE_BLOCKS], F32)
 
         def bias_transpose():
-            bias_bank = bank_pool.tile([P, 2 * BANK_WORDS], BF16, tag="bank")
+            bias_bank = bank_tile([P, 2 * BANK_WORDS], BF16)
             nc.tensor.transpose(bias_bank[:, 0:P], bias_rows[:], ident_bf16[:])
-            nc.vector.tensor_copy(out=bias_cols[:], in_=bias_bank[:, 0 : ROW_BLOCKS + BLOCKS_PER_GATE])
+            nc.vector.tensor_copy(out=bias_cols[:], in_=bias_bank[:, 0 : ROW_BLOCKS + GATE_BLOCKS])
+            nc.vector.tensor_scalar_mul(out=bias_neg[:], in0=bias_cols[:], scalar1=-1.0)
 
         whh_codes = keep.tile([P, ROW_BLOCKS * P], U32, align_bytes=64)
         whh_scales = keep.tile([P, ROW_BLOCKS * P], U8, align_bytes=64)
+        h_codes = keep.tile([P, 16 * BATCH], U32, align_bytes=64)
+        h_scales = keep.tile([P, 16 * BATCH], U8, align_bytes=64)
+        w_codes = {}
+        w_scales = {}
+        groups = {}
+        accs = {}
 
-        def whh_transposes():
-            words = whh_sb[:].bitcast(F32)
-            groups = []
-            for piece in range(ROW_BLOCKS // 4):
-                blocks = [words[:, P * i : P * (i + 1)] for i in range(8 * piece, 8 * piece + 8)]
-                groups.append(transpose_and_group(blocks, 2, 1 if piece % 2 == 0 else None))
-            return groups
+        def transposes(item):
+            kind, a, c = item
+            if kind == "h":
+                words = [piece.bitcast(F32) for piece in raw[item]]
+                groups[item] = []
+                for half in range(2):
+                    blocks = [
+                        words[t][:, 256 * g + P * u : 256 * g + P * (u + 1)]
+                        for g in (2 * half, 2 * half + 1)
+                        for u in range(2)
+                        for t in range(2)
+                    ]
+                    groups[item].append(transpose_and_group(blocks, 1))
+            else:
+                words = raw[item][0].bitcast(F32)
+                groups[item] = [transpose_and_group([words[:, P * b : P * (b + 1)] for b in range(8)], 2)]
 
-        def whh_quantise(groups):
-            for piece in range(ROW_BLOCKS // 4):
-                cols = slice(4 * P * piece, 4 * P * (piece + 1))
-                quantise(groups[piece], whh_codes[:, cols], whh_scales[:, cols])
+        def quantises(item):
+            kind, a, c = item
+            if kind == "whh":
+                cols = slice(4 * P * a, 4 * P * (a + 1))
+                quantise(groups[item][0], whh_codes[:, cols], whh_scales[:, cols])
+            elif kind == "h":
+                for half in range(2):
+                    cols = slice(BATCH * (4 * a + 2 * half), BATCH * (4 * a + 2 * half + 2))
+                    quantise(groups[item][half], h_codes[:, cols], h_scales[:, cols])
+            else:
+                codes = code_pool.tile([P, QUARTER_PASSES * P], U32, align_bytes=64, tag="codes")
+                scales = code_pool.tile([P, QUARTER_PASSES * P], U8, align_bytes=64, tag="scales")
+                quantise(groups[item][0], codes[:], scales[:])
+                w_codes[item] = codes
+                w_scales[item] = scales
 
         def hh_pass(acc, j, start, stop):
             cols = slice(P * j, P * (j + 1))
             mx_pass(acc, whh_codes[:, cols], whh_scales[:, cols], prev_codes[:], prev_scales[:], start, stop)
 
-        h_codes = {}
-        h_scales = {}
-
-        def h_transposes(c):
-            words = h_sb[c][:].bitcast(F32)
-            groups = []
-            for piece in range(2):
-                blocks = [
-                    words[:, 1024 * t + 256 * g + P * u : 1024 * t + 256 * g + P * (u + 1)]
-                    for g in (2 * piece, 2 * piece + 1)
-                    for u in range(2)
-                    for t in range(2)
-                ]
-                groups.append(transpose_and_group(blocks, 1, 1 if piece == 0 else None))
-            return groups
-
-        def h_quantise(c, groups):
-            codes = h_pool.tile([P, QUARTER_PASSES * BATCH], U32, align_bytes=64)
-            scales = h_pool.tile([P, QUARTER_PASSES * BATCH], U8, align_bytes=64)
-            for piece in range(2):
-                cols = slice(2 * BATCH * piece, 2 * BATCH * (piece + 1))
-                quantise(groups[piece], codes[:, cols], scales[:, cols])
-            h_codes[c] = codes
-            h_scales[c] = scales
-
-        w_codes = {}
-        w_scales = {}
-        accs = {}
-
-        def w_transposes(step):
-            pair, c = divmod(step, QUARTERS)
-            groups = []
-            for i in range(2):
-                words = w_sb[(2 * pair + i, c)][:].bitcast(F32)
-                blocks = [words[:, P * b : P * (b + 1)] for b in range(8)]
-                groups.append(transpose_and_group(blocks, 2, 1 if i == 0 else None))
-            return groups
-
-        def w_quantise(step, groups):
-            pair, c = divmod(step, QUARTERS)
-            for i in range(2):
-                codes = code_pool.tile([P, QUARTER_PASSES * P], U32, align_bytes=64)
-                scales = code_pool.tile([P, QUARTER_PASSES * P], U8, align_bytes=64)
-                quantise(groups[i], codes[:], scales[:])
-                w_codes[(2 * pair + i, c)] = codes
-                w_scales[(2 * pair + i, c)] = scales
-
-        def w_passes(step):
-            pair, c = divmod(step, QUARTERS)
-            for j in (2 * pair, 2 * pair + 1):
-                sums_hh = j < 2 * BLOCKS_PER_GATE
-                if c == 0:
-                    acc = acc_pool.tile([P, BATCH], F32)
-                    accs[j] = acc
-                for s in range(QUARTER_PASSES):
-                    g = QUARTER_PASSES * c + s
-                    mx_pass(
-                        accs[j][:],
-                        w_codes[(j, c)][:, P * s : P * (s + 1)],
-                        w_scales[(j, c)][:, P * s : P * (s + 1)],
-                        h_codes[c][:, BATCH * s : BATCH * (s + 1)],
-                        h_scales[c][:, BATCH * s : BATCH * (s + 1)],
-                        g == 0,
-                        g == PASSES - 1 and not sums_hh,
-                    )
-                if c == QUARTERS - 1 and sums_hh:
-                    hh_pass(accs[j][:], j, False, True)
-
-        hn_b = keep.tile([P, BLOCKS_PER_GATE * BATCH], F32)
-        reset_hn = keep.tile([P, BLOCKS_PER_GATE * BATCH], F32)
-        update_prev = keep.tile([P, BLOCKS_PER_GATE * BATCH], F32)
-        one_less_update = keep.tile([P, BLOCKS_PER_GATE * BATCH], F32)
-        results = {}
+        hn_b = keep.tile([P, GATE_BLOCKS * BATCH], F32)
+        reset_hn = keep.tile([P, GATE_BLOCKS * BATCH], F32)
+        d_row = keep.tile([P, GATE_BLOCKS * BATCH], F32)
+        prev_rows = prev_sb[:].rearrange("p (t k) -> p t k", t=2)
 
         def hn_products():
-            for half in range(BLOCKS_PER_GATE // 2):
-                hn_bank = bank_pool.tile([P, BANK_WORDS], F32, tag="bank")
+            for half in range(2):
+                hn_bank = bank_tile([P, BANK_WORDS], F32)
                 for i in range(2):
-                    f = 2 * half + i
-                    hh_pass(hn_bank[:, BATCH * i : BATCH * (i + 1)], 2 * BLOCKS_PER_GATE + f, True, True)
+                    hh_pass(hn_bank[:, BATCH * i : BATCH * (i + 1)], 2 * GATE_BLOCKS + 2 * half + i, True, True)
                 for i in range(2):
                     f = 2 * half + i
                     nc.scalar.activation(
-                        out=hn_b[:, BATCH * f : BATCH * (f + 1)],
-                        in_=hn_bank[:, BATCH * i : BATCH * (i + 1)],
-                        func=ACT.Identity,
-                        bias=bias_cols[:, ROW_BLOCKS + f : ROW_BLOCKS + f + 1],
+                        out=hn_b[:, BATCH * f : BATCH * (f + 1)], in_=hn_bank[:, BATCH * i : BATCH * (i + 1)],
+                        func=ACT.Identity, bias=bias_cols[:, ROW_BLOCKS + f : ROW_BLOCKS + f + 1],
                     )
 
-        def gate_columns(j):
-            f = j % BLOCKS_PER_GATE
-            return slice(BATCH * f, BATCH * (f + 1))
+        to_turn = []
+        acc_count = [0]
+        acc_tiles = {}
 
-        def sigmoid_of(j):
-            gate = work.tile([P, BATCH], F32)
-            nc.scalar.activation(out=gate[:], in_=accs[j][:], func=ACT.Sigmoid, bias=bias_cols[:, j : j + 1])
-            return gate
+        def new_acc():
+            k = acc_count[0]
+            acc_count[0] += 1
+            if k < HEAD_BLOCKS:
+                per_bank = HEAD_BLOCKS // ACC_BANKS_HEAD
+                index, half = divmod(k, per_bank)
+                if half == 0:
+                    acc_bank = psum.tile([P, BANK_WORDS], F32, tag="bank%d" % index)
+                    acc_tiles[index] = acc_bank
+                return acc_tiles[index][:, BATCH * half : BATCH * (half + 1)]
+            if k == HEAD_BLOCKS:
+                for index in range(ACC_BANKS_LATER, ACC_BANKS_HEAD):
+                    turn_banks.append(index)
+            index = (k - HEAD_BLOCKS) % ACC_BANKS_LATER
+            acc_bank = psum.tile([P, BANK_WORDS], F32, tag="bank%d" % index)
+            return acc_bank[:, 0:BATCH]
 
-        def gates(pair):
-            blocks = (2 * pair, 2 * pair + 1)
-            kind = blocks[0] // BLOCKS_PER_GATE
+        def passes(item):
+            kind, j, c = item
+            sums_hh = j < 2 * GATE_BLOCKS
+            if c == 0:
+                accs[j] = new_acc()
+                if sums_hh:
+                    hh_pass(accs[j], j, True, False)
+            for s in range(QUARTER_PASSES):
+                g = QUARTER_PASSES * c + s
+                mx_pass(
+                    accs[j], w_codes[item][:, P * s : P * (s + 1)], w_scales[item][:, P * s : P * (s + 1)],
+                    h_codes[:, BATCH * g : BATCH * (g + 1)], h_scales[:, BATCH * g : BATCH * (g + 1)],
+                    g == 0 and not sums_hh, g == 15,
+                )
+            if c == QUARTERS - 1:
+                gate(j)
+
+        def gate(j):
+            kind, f = divmod(j, GATE_BLOCKS)
+            cols = slice(BATCH * f, BATCH * (f + 1))
             if kind == 0:
-                resets = [sigmoid_of(j) for j in blocks]
-                for i in range(2):
-                    cols = gate_columns(blocks[i])
-                    nc.vector.tensor_tensor(out=reset_hn[:, cols], in0=hn_b[:, cols], in1=resets[i][:], op=ALU.mult)
-            elif kind == 1:
-                updates = [sigmoid_of(j) for j in blocks]
-                for i in range(2):
-                    cols = gate_columns(blocks[i])
-                    nc.vector.tensor_tensor(out=update_prev[:, cols], in0=updates[i][:], in1=prev_t[:, cols], op=ALU.mult)
-                    nc.vector.tensor_scalar(
-                        out=one_less_update[:, cols],
-                        in0=updates[i][:],
-                        scalar1=-1.0,
-                        scalar2=1.0,
-                        op0=ALU.mult,
-                        op1=ALU.add,
-                    )
+                reset = work.tile([P, BATCH], F32, tag="reset")
+                nc.scalar.activation(out=reset[:], in_=accs[j], func=ACT.Sigmoid, bias=bias_cols[:, j : j + 1])
+                nc.vector.tensor_tensor(out=reset_hn[:, cols], in0=hn_b[:, cols], in1=reset[:], op=ALU.mult)
+            elif kind == 2:
+                pre = work.tile([P, BATCH], F32, tag="pre")
+                nc.vector.tensor_tensor(out=pre[:], in0=accs[j], in1=reset_hn[:, cols], op=ALU.add)
+                new = work.tile([P, BATCH], F32, tag="new")
+                nc.scalar.activation(out=new[:], in_=pre[:], func=ACT.Tanh, bias=bias_cols[:, j : j + 1])
+                to_turn.append((j, new))
             else:
-                news = []
-                for j in blocks:
-                    pre = work.tile([P, BATCH], F32)
-                    nc.vector.tensor_tensor(out=pre[:], in0=accs[j][:], in1=reset_hn[:, gate_columns(j)], op=ALU.add)
-                    new = work.tile([P, BATCH], F32)
-                    nc.scalar.activation(out=new[:], in_=pre[:], func=ACT.Tanh, bias=bias_cols[:, j : j + 1])
-                    news.append(new)
-                for i in range(2):
-                    cols = gate_columns(blocks[i])
-                    kept = work.tile([P, BATCH], F32)
-                    nc.vector.tensor_tensor(out=kept[:], in0=news[i][:], in1=one_less_update[:, cols], op=ALU.mult)
-                    result = work.tile([P, BATCH], F32, bufs=BLOCKS_PER_GATE)
-                    nc.vector.tensor_tensor(out=result[:], in0=kept[:], in1=update_prev[:, cols], op=ALU.add)
-                    results[blocks[i] % BLOCKS_PER_GATE] = result
+                keepn = work.tile([P, BATCH], F32, tag="keepn")
+                nc.scalar.activation(out=keepn[:], in_=accs[j], func=ACT.Sigmoid, bias=bias_neg[:, j : j + 1], scale=-1.0)
+                to_turn.append((j, keepn))
 
-        def store_block(f):
-            back = bank_pool.tile([P, BANK_WORDS], F32, tag="bank")
-            for t in range(2):
-                nc.tensor.transpose(back[:, P * t : P * (t + 1)], results[f][:, P * t : P * (t + 1)], ident_f32[:])
-            out_sb = work.tile([P, BATCH], F32)
-            nc.scalar.copy(out=out_sb[:], in_=back[:, 0:BATCH])
-            nc.sync.dma_start(
-                out=out.rearrange("(t p) r -> p t r", p=P)[:, :, P * f : P * (f + 1)],
-                in_=out_sb[:].rearrange("p (t r) -> p t r", t=2),
-            )
+        def turn_back():
+            for j, turned in to_turn:
+                kind, f = divmod(j, GATE_BLOCKS)
+                cols = slice(BATCH * f, BATCH * (f + 1))
+                back = bank_tile([P, BANK_WORDS], F32)
+                for t in range(2):
+                    nc.tensor.transpose(back[:, P * t : P * (t + 1)], turned[:, P * t : P * (t + 1)], ident_f32[:])
+                prev_f = prev_rows[:, :, P * f : P * (f + 1)]
+                if kind == 2:
+                    nc.vector.tensor_tensor(
+                        out=d_row[:, cols].rearrange("p (t r) -> p t r", t=2), in0=prev_f,
+                        in1=back[:, 0:BATCH].rearrange("p (t r) -> p t r", t=2), op=ALU.subtract,
+                    )
+                else:
+                    moved = work.tile([P, BATCH], F32, tag="moved")
+                    nc.vector.tensor_tensor(out=moved[:], in0=back[:, 0:BATCH], in1=d_row[:, cols], op=ALU.mult)
+                    out_sb = work.tile([P, BATCH], F32, tag="out_sb")
+                    nc.vector.tensor_tensor(
+                        out=out_sb[:].rearrange("p (t r) -> p t r", t=2), in0=prev_f,
+                        in1=moved[:].rearrange("p (t r) -> p t r", t=2), op=ALU.subtract,
+                    )
+                    nc.sync.dma_start(
+                        out=out.rearrange("(t p) r -> p t r", p=P)[:, :, P * f : P * (f + 1)],
+                        in_=out_sb[:].rearrange("p (t r) -> p t r", t=2),
+                    )
+            to_turn.clear()
 
-        runs = [[step] for step in range(QUARTERS)]
-        runs += [list(range(step, step + RUN_STEPS)) for step in range(QUARTERS, STEPS, RUN_STEPS)]
-        for i in range(len(runs) + 1):
-            if i < len(runs):
-                for step in runs[i]:
-                    if step < QUARTERS:
-                        h_groups = h_transposes(step)
-                    w_groups = w_transposes(step)
-                    if step + STEPS_AHEAD < STEPS:
-                        load_w(step + STEPS_AHEAD)
-                    if step < QUARTERS:
-                        h_quantise(step, h_groups)
-                    w_quantise(step, w_groups)
-                    if step == 0:
-                        bias_transpose()
-                        whh_quantise(whh_transposes())
-            if i == len(runs) - 1:
-                store_block(0)
-                store_block(1)
-            if i == 1:
-                hn_products()
-            if i >= 1:
-                for step in runs[i - 1]:
-                    w_passes(step)
-                    if step % QUARTERS == QUARTERS - 1:
-                        gates(step // QUARTERS)
-        store_block(2)
-        store_block(3)
+        units = [items[0:3]] + [u for c in range(QUARTERS) for u in (items[3 + 3 * c : 4 + 3 * c], items[4 + 3 * c : 6 + 3 * c])] + [items[k : k + 4] for k in range(15, len(items), 4)]
+        quantise(prev_grouped, prev_codes[:], prev_scales[:])
+        done_items = [0]
+        for i in range(len(units) + LAG):
+            if i < len(units):
+                for item in units[i]:
+                    transposes(item)
+                    done_items[0] += 1
+                    load_ahead(done_items[0] + AHEAD)
+                if i == 0:
+                    bias_transpose()
+                turn_back()
+                for item in units[i]:
+                    quantises(item)
+            if i >= LAG:
+                for item in units[i - LAG]:
+                    if item == ("whh", 2, 0):
+                        hn_products()
+                    if item[0] == "w":
+                        passes(item)
+        turn_back()

@@ -30,6 +30,7 @@ HEAD_BLOCKS = 2
 ACC_BANKS_HEAD = 2
 ACC_BANKS_LATER = 2
 LAG = 1
+QLAG = 1
 
 FLOPS = 2 * BATCH * 3 * HIDDEN * (K_IH + HIDDEN)
 
@@ -159,6 +160,16 @@ def tile_prior_pa_k_kernel(tc, h, prev_rnn_hidden, W_ih, W_hh, b_ih, b_n, out):
         prev_scales = keep.tile([P, BATCH], U8, align_bytes=64)
         prev_blocks = [prev_words[:, 256 * t + P * u : 256 * t + P * (u + 1)] for u in range(2) for t in range(2)]
         prev_grouped = transpose_and_group(prev_blocks, 1)
+        prev_t_bank = bank_tile([P, 2 * BANK_WORDS], BF16)
+        for f in range(GATE_BLOCKS):
+            for t in range(2):
+                nc.tensor.transpose(
+                    prev_t_bank[:, BATCH * f + P * t : BATCH * f + P * (t + 1)],
+                    prev_sb[:, HIDDEN * t + P * f : HIDDEN * t + P * (f + 1)],
+                    ident_bf16[:],
+                )
+        prev_t = keep.tile([P, GATE_BLOCKS * BATCH], F32)
+        nc.scalar.copy(out=prev_t[:], in_=prev_t_bank[:])
         bias_cols = keep.tile([P, ROW_BLOCKS + GATE_BLOCKS], F32)
         bias_neg = keep.tile([P, ROW_BLOCKS + GATE_BLOCKS], F32)
 
@@ -216,7 +227,7 @@ def tile_prior_pa_k_kernel(tc, h, prev_rnn_hidden, W_ih, W_hh, b_ih, b_n, out):
 
         hn_b = keep.tile([P, GATE_BLOCKS * BATCH], F32)
         reset_hn = keep.tile([P, GATE_BLOCKS * BATCH], F32)
-        d_row = keep.tile([P, GATE_BLOCKS * BATCH], F32)
+        d_col = keep.tile([P, GATE_BLOCKS * BATCH], F32)
         prev_rows = prev_sb[:].rearrange("p (t k) -> p t k", t=2)
 
         def hn_products():
@@ -281,11 +292,13 @@ def tile_prior_pa_k_kernel(tc, h, prev_rnn_hidden, W_ih, W_hh, b_ih, b_n, out):
                 nc.vector.tensor_tensor(out=pre[:], in0=accs[j], in1=reset_hn[:, cols], op=ALU.add)
                 new = work.tile([P, BATCH], F32, tag="new")
                 nc.scalar.activation(out=new[:], in_=pre[:], func=ACT.Tanh, bias=bias_cols[:, j : j + 1])
-                to_turn.append((j, new))
+                nc.vector.tensor_tensor(out=d_col[:, cols], in0=prev_t[:, cols], in1=new[:], op=ALU.subtract)
             else:
                 keepn = work.tile([P, BATCH], F32, tag="keepn")
                 nc.scalar.activation(out=keepn[:], in_=accs[j], func=ACT.Sigmoid, bias=bias_neg[:, j : j + 1], scale=-1.0)
-                to_turn.append((j, keepn))
+                moved = work.tile([P, BATCH], F32, tag="moved")
+                nc.vector.tensor_tensor(out=moved[:], in0=keepn[:], in1=d_col[:, cols], op=ALU.mult)
+                to_turn.append((j, moved))
 
         def turn_back():
             for j, turned in to_turn:
@@ -295,23 +308,15 @@ def tile_prior_pa_k_kernel(tc, h, prev_rnn_hidden, W_ih, W_hh, b_ih, b_n, out):
                 for t in range(2):
                     nc.tensor.transpose(back[:, P * t : P * (t + 1)], turned[:, P * t : P * (t + 1)], ident_f32[:])
                 prev_f = prev_rows[:, :, P * f : P * (f + 1)]
-                if kind == 2:
-                    nc.vector.tensor_tensor(
-                        out=d_row[:, cols].rearrange("p (t r) -> p t r", t=2), in0=prev_f,
-                        in1=back[:, 0:BATCH].rearrange("p (t r) -> p t r", t=2), op=ALU.subtract,
-                    )
-                else:
-                    moved = work.tile([P, BATCH], F32, tag="moved")
-                    nc.vector.tensor_tensor(out=moved[:], in0=back[:, 0:BATCH], in1=d_row[:, cols], op=ALU.mult)
-                    out_sb = work.tile([P, BATCH], F32, tag="out_sb")
-                    nc.vector.tensor_tensor(
-                        out=out_sb[:].rearrange("p (t r) -> p t r", t=2), in0=prev_f,
-                        in1=moved[:].rearrange("p (t r) -> p t r", t=2), op=ALU.subtract,
-                    )
-                    nc.sync.dma_start(
-                        out=out.rearrange("(t p) r -> p t r", p=P)[:, :, P * f : P * (f + 1)],
-                        in_=out_sb[:].rearrange("p (t r) -> p t r", t=2),
-                    )
+                out_sb = work.tile([P, BATCH], F32, tag="out_sb")
+                nc.vector.tensor_tensor(
+                    out=out_sb[:].rearrange("p (t r) -> p t r", t=2), in0=prev_f,
+                    in1=back[:, 0:BATCH].rearrange("p (t r) -> p t r", t=2), op=ALU.subtract,
+                )
+                nc.sync.dma_start(
+                    out=out.rearrange("(t p) r -> p t r", p=P)[:, :, P * f : P * (f + 1)],
+                    in_=out_sb[:].rearrange("p (t r) -> p t r", t=2),
+                )
             to_turn.clear()
 
         units = [items[0:3]] + [u for c in range(QUARTERS) for u in (items[3 + 3 * c : 4 + 3 * c], items[4 + 3 * c : 6 + 3 * c])] + [items[k : k + 4] for k in range(15, len(items), 4)]
@@ -319,14 +324,16 @@ def tile_prior_pa_k_kernel(tc, h, prev_rnn_hidden, W_ih, W_hh, b_ih, b_n, out):
         done_items = [0]
         for i in range(len(units) + LAG):
             if i < len(units):
-                for item in units[i]:
+                for k, item in enumerate(units[i]):
                     transposes(item)
                     done_items[0] += 1
                     load_ahead(done_items[0] + AHEAD)
+                    if k >= QLAG:
+                        quantises(units[i][k - QLAG])
                 if i == 0:
                     bias_transpose()
                 turn_back()
-                for item in units[i]:
+                for item in units[i][max(0, len(units[i]) - QLAG) :]:
                     quantises(item)
             if i >= LAG:
                 for item in units[i - LAG]:

@@ -23,14 +23,18 @@ QUARTERS = 4
 QUARTER = K_IH // QUARTERS
 QUARTER_PASSES = QUARTER // K_PASS
 RAW_BUFS = 24
+RAW1_BUFS = 12
+RAWB_BUFS = 7
 LPH = 1
-LPB = 1
+LPB = 2
 AHEAD = 16
 HEAD_BLOCKS = 2
 ACC_BANKS_HEAD = 2
 ACC_BANKS_LATER = 2
 LAG = 1
 QLAG = 1
+VMOD = 4
+SPAN = 1
 
 FLOPS = 2 * BATCH * 3 * HIDDEN * (K_IH + HIDDEN)
 
@@ -79,7 +83,10 @@ def tile_prior_pa_k_kernel(tc, h, prev_rnn_hidden, W_ih, W_hh, b_ih, b_n, out):
             for j in head:
                 items += [("w", j, c) for c in range(c0, c0 + LPH)]
         for j in block_order[HEAD_BLOCKS:]:
-            items += [("w", j, c) for c in range(QUARTERS)]
+            items += [("w", j, c) for c in range(0, QUARTERS, SPAN)]
+
+        def span(item):
+            return 1 if item[1] in head else SPAN
 
         raw = {}
         prev_sb = keep.tile([P, 2 * HIDDEN], BF16)
@@ -88,48 +95,64 @@ def tile_prior_pa_k_kernel(tc, h, prev_rnn_hidden, W_ih, W_hh, b_ih, b_n, out):
             in_=prev_rnn_hidden.rearrange("(t p) k -> p t k", p=P),
         )
 
-        def load(item):
-            kind, a, c = item
+        loads = []
+        for kind, a, c in items:
             if kind == "whh":
-                piece = raw_pool.tile([P, QUARTER], BF16, tag="raw1")
+                loads.append((kind, a, 0, 1))
+            elif kind == "h" and a % LPH == 0:
+                loads += [(kind, t, a, LPH) for t in range(2)]
+            elif kind == "w" and a in head and c % LPH == 0:
+                loads.append((kind, a, c, LPH))
+            elif kind == "w" and a not in head and c % LPB == 0:
+                loads.append((kind, a, c, LPB))
+        raw_bufs = {1: RAW1_BUFS, LPB: RAWB_BUFS}
+        in_use = {1: 0, LPB: 0}
+        quarters_left = {}
+        next_load = [0]
+
+        def issue(load):
+            kind, a, c, width = load
+            piece = raw_pool.tile([P, width * QUARTER], BF16, tag="raw%d" % width, bufs=raw_bufs[width])
+            if kind == "whh":
                 nc.sync.dma_start(
                     out=piece[:].rearrange("p (j k) -> p j k", j=4),
                     in_=W_hh[4 * P * a : 4 * P * (a + 1), :].rearrange("(j p) k -> p j k", p=P),
                 )
-                raw[item] = [piece[:]]
-                return
-            lp = LPH if (kind == "h" or a in head) else LPB
-            q = a if kind == "h" else c
-            if q % lp != 0:
-                return
-            if kind == "h":
-                for cc in range(q, q + lp):
-                    raw[("h", cc, 0)] = []
-                for t in range(2):
-                    piece = raw_pool.tile([P, lp * QUARTER], BF16, tag="raw%d" % lp, bufs=RAW_BUFS // lp)
-                    nc.sync.dma_start(out=piece[:], in_=h[P * t : P * (t + 1), QUARTER * q : QUARTER * (q + lp)])
-                    for i in range(lp):
-                        raw[("h", q + i, 0)].append(piece[:, QUARTER * i : QUARTER * (i + 1)])
+                raw[(kind, a, 0)] = [piece[:]]
             else:
-                piece = raw_pool.tile([P, lp * QUARTER], BF16, tag="raw%d" % lp, bufs=RAW_BUFS // lp)
-                nc.sync.dma_start(out=piece[:], in_=W_ih[P * a : P * (a + 1), QUARTER * q : QUARTER * (q + lp)])
-                for i in range(lp):
-                    raw[("w", a, q + i)] = [piece[:, QUARTER * i : QUARTER * (i + 1)]]
+                source = h if kind == "h" else W_ih
+                nc.sync.dma_start(out=piece[:], in_=source[P * a : P * (a + 1), QUARTER * c : QUARTER * (c + width)])
+                for i in range(width):
+                    part = piece[:, QUARTER * i : QUARTER * (i + 1)]
+                    if kind == "h":
+                        raw.setdefault((kind, c + i, 0), []).append(part)
+                    else:
+                        raw[(kind, a, c + i)] = [part]
+            quarters_left[load] = width
 
-        loaded = [0]
+        def load_ahead():
+            for index in range(next_load[0], len(loads)):
+                width = loads[index][3]
+                if in_use[width] >= raw_bufs[width]:
+                    return
+                issue(loads[index])
+                in_use[width] += 1
+                next_load[0] = index + 1
 
-        def load_ahead(upto):
-            for index in range(loaded[0], min(len(items), upto)):
-                load(items[index])
-                loaded[0] = index + 1
+        def release(kind, a, c):
+            for load in loads[: next_load[0]]:
+                if load[0] == kind and load[1] == a and load[2] <= c < load[2] + load[3]:
+                    quarters_left[load] -= 1
+                    if quarters_left[load] == 0:
+                        in_use[load[3]] -= 1
 
-        load_ahead(AHEAD)
+        load_ahead()
 
         banks_used = [0]
 
         def transpose_and_group(blocks, slabs):
             banks = len(blocks) // 4
-            grouped = group_pool.tile([P, 2 * BANK_WORDS * banks], BF16, align_bytes=64, tag="grouped")
+            grouped = group_pool.tile([P, 2 * BANK_WORDS * banks], BF16, align_bytes=64, tag="grouped%d" % ((banks + 1) // 2))
             grouped_words = grouped[:].bitcast(F32)
             for b in range(banks):
                 bank = bank_tile([P, BANK_WORDS], F32)
@@ -139,7 +162,7 @@ def tile_prior_pa_k_kernel(tc, h, prev_rnn_hidden, W_ih, W_hh, b_ih, b_n, out):
                 dst = grouped_words[:, BANK_WORDS * b : BANK_WORDS * (b + 1)].rearrange(
                     "p (s c u) -> p s c u", s=slabs, u=2
                 )
-                if banks_used[0] % 4 == 1:
+                if banks_used[0] % VMOD == 1:
                     nc.vector.tensor_copy(out=dst, in_=src)
                 else:
                     nc.scalar.copy(out=dst, in_=src)
@@ -202,8 +225,9 @@ def tile_prior_pa_k_kernel(tc, h, prev_rnn_hidden, W_ih, W_hh, b_ih, b_n, out):
                     ]
                     groups[item].append(transpose_and_group(blocks, 1))
             else:
-                words = raw[item][0].bitcast(F32)
-                groups[item] = [transpose_and_group([words[:, P * b : P * (b + 1)] for b in range(8)], 2)]
+                quarters = [c] if kind == "whh" else list(range(c, c + span(item)))
+                words = [raw[(kind, a, q)][0].bitcast(F32) for q in quarters]
+                groups[item] = [transpose_and_group([w[:, P * b : P * (b + 1)] for w in words for b in range(8)], 2)]
 
         def quantises(item):
             kind, a, c = item
@@ -215,8 +239,8 @@ def tile_prior_pa_k_kernel(tc, h, prev_rnn_hidden, W_ih, W_hh, b_ih, b_n, out):
                     cols = slice(BATCH * (4 * a + 2 * half), BATCH * (4 * a + 2 * half + 2))
                     quantise(groups[item][half], h_codes[:, cols], h_scales[:, cols])
             else:
-                codes = code_pool.tile([P, QUARTER_PASSES * P], U32, align_bytes=64, tag="codes")
-                scales = code_pool.tile([P, QUARTER_PASSES * P], U8, align_bytes=64, tag="scales")
+                codes = code_pool.tile([P, span(item) * QUARTER_PASSES * P], U32, align_bytes=64, tag="codes%d" % span(item))
+                scales = code_pool.tile([P, span(item) * QUARTER_PASSES * P], U8, align_bytes=64, tag="scales%d" % span(item))
                 quantise(groups[item][0], codes[:], scales[:])
                 w_codes[item] = codes
                 w_scales[item] = scales
@@ -270,14 +294,14 @@ def tile_prior_pa_k_kernel(tc, h, prev_rnn_hidden, W_ih, W_hh, b_ih, b_n, out):
                 accs[j] = new_acc()
                 if sums_hh:
                     hh_pass(accs[j], j, True, False)
-            for s in range(QUARTER_PASSES):
+            for s in range(span(item) * QUARTER_PASSES):
                 g = QUARTER_PASSES * c + s
                 mx_pass(
                     accs[j], w_codes[item][:, P * s : P * (s + 1)], w_scales[item][:, P * s : P * (s + 1)],
                     h_codes[:, BATCH * g : BATCH * (g + 1)], h_scales[:, BATCH * g : BATCH * (g + 1)],
                     g == 0 and not sums_hh, g == 15,
                 )
-            if c == QUARTERS - 1:
+            if c + span(item) == QUARTERS:
                 gate(j)
 
         def gate(j):
@@ -295,9 +319,19 @@ def tile_prior_pa_k_kernel(tc, h, prev_rnn_hidden, W_ih, W_hh, b_ih, b_n, out):
                 nc.vector.tensor_tensor(out=d_col[:, cols], in0=prev_t[:, cols], in1=new[:], op=ALU.subtract)
             else:
                 keepn = work.tile([P, BATCH], F32, tag="keepn")
-                nc.scalar.activation(out=keepn[:], in_=accs[j], func=ACT.Sigmoid, bias=bias_neg[:, j : j + 1], scale=-1.0)
                 moved = work.tile([P, BATCH], F32, tag="moved")
-                nc.vector.tensor_tensor(out=moved[:], in0=keepn[:], in1=d_col[:, cols], op=ALU.mult)
+                parts = 2 if j == block_order[-1] else 1
+                width = BATCH // parts
+                for i in range(parts):
+                    part = slice(width * i, width * (i + 1))
+                    nc.scalar.activation(
+                        out=keepn[:, part], in_=accs[j][:, part], func=ACT.Sigmoid, bias=bias_neg[:, j : j + 1], scale=-1.0
+                    )
+                for i in range(parts):
+                    part = slice(width * i, width * (i + 1))
+                    nc.vector.tensor_tensor(
+                        out=moved[:, part], in0=keepn[:, part], in1=d_col[:, BATCH * f + width * i : BATCH * f + width * (i + 1)], op=ALU.mult
+                    )
                 to_turn.append((j, moved))
 
         def turn_back():
@@ -307,16 +341,24 @@ def tile_prior_pa_k_kernel(tc, h, prev_rnn_hidden, W_ih, W_hh, b_ih, b_n, out):
                 back = bank_tile([P, BANK_WORDS], F32)
                 for t in range(2):
                     nc.tensor.transpose(back[:, P * t : P * (t + 1)], turned[:, P * t : P * (t + 1)], ident_f32[:])
-                prev_f = prev_rows[:, :, P * f : P * (f + 1)]
                 out_sb = work.tile([P, BATCH], F32, tag="out_sb")
-                nc.vector.tensor_tensor(
-                    out=out_sb[:].rearrange("p (t r) -> p t r", t=2), in0=prev_f,
-                    in1=back[:, 0:BATCH].rearrange("p (t r) -> p t r", t=2), op=ALU.subtract,
-                )
-                nc.sync.dma_start(
-                    out=out.rearrange("(t p) r -> p t r", p=P)[:, :, P * f : P * (f + 1)],
-                    in_=out_sb[:].rearrange("p (t r) -> p t r", t=2),
-                )
+                if j == block_order[-1]:
+                    for t in range(2):
+                        nc.vector.tensor_tensor(
+                            out=out_sb[:, P * t : P * (t + 1)], in0=prev_sb[:, HIDDEN * t + P * f : HIDDEN * t + P * (f + 1)],
+                            in1=back[:, P * t : P * (t + 1)], op=ALU.subtract,
+                        )
+                        nc.sync.dma_start(out=out[P * t : P * (t + 1), P * f : P * (f + 1)], in_=out_sb[:, P * t : P * (t + 1)])
+                else:
+                    prev_f = prev_rows[:, :, P * f : P * (f + 1)]
+                    nc.vector.tensor_tensor(
+                        out=out_sb[:].rearrange("p (t r) -> p t r", t=2), in0=prev_f,
+                        in1=back[:, 0:BATCH].rearrange("p (t r) -> p t r", t=2), op=ALU.subtract,
+                    )
+                    nc.sync.dma_start(
+                        out=out.rearrange("(t p) r -> p t r", p=P)[:, :, P * f : P * (f + 1)],
+                        in_=out_sb[:].rearrange("p (t r) -> p t r", t=2),
+                    )
             to_turn.clear()
 
         units = [items[0:3]] + [u for c in range(QUARTERS) for u in (items[3 + 3 * c : 4 + 3 * c], items[4 + 3 * c : 6 + 3 * c])] + [items[k : k + 4] for k in range(15, len(items), 4)]
@@ -326,8 +368,13 @@ def tile_prior_pa_k_kernel(tc, h, prev_rnn_hidden, W_ih, W_hh, b_ih, b_n, out):
             if i < len(units):
                 for k, item in enumerate(units[i]):
                     transposes(item)
-                    done_items[0] += 1
-                    load_ahead(done_items[0] + AHEAD)
+                    if item[0] == "h":
+                        release("h", 0, item[1])
+                        release("h", 1, item[1])
+                    else:
+                        for q in range(item[2], item[2] + (1 if item[0] == "whh" else span(item))):
+                            release(item[0], item[1], q)
+                    load_ahead()
                     if k >= QLAG:
                         quantises(units[i][k - QLAG])
                 if i == 0:

from contextlib import ExitStack

import concourse.mybir as mybir
from concourse.masks import make_identity

F32 = mybir.dt.float32
BF16 = mybir.dt.bfloat16
U32 = mybir.dt.uint32
U8 = mybir.dt.uint8
FP8X4 = mybir.dt.float8_e4m3fn_x4
ACT = mybir.ActivationFunctionType
ALU = mybir.AluOpType

P = 128
BATCH = 256
HIDDEN = 512
K_IH = 8192
K_PASS = 512
ROW_BLOCKS = 12
GATE_BLOCKS = 4
BANK_WORDS = 512
QUARTERS = 4
QUARTER = K_IH // QUARTERS
QUARTER_PASSES = QUARTER // K_PASS
RAW_BUFS = 24
RAW1_BUFS = 12
RAWB_BUFS = 7
LPH = 1
LPB = 2
AHEAD = 16
HEAD_BLOCKS = 2
ACC_BANKS_HEAD = 2
ACC_BANKS_LATER = 2
LAG = 1
QLAG = 1
VMOD = 4
SPAN = 1

FLOPS = 2 * BATCH * 3 * HIDDEN * (K_IH + HIDDEN)


def tile_prior_pa_k_kernel(tc, h, prev_rnn_hidden, W_ih, W_hh, b_ih, b_n, out):
    nc = tc.nc
    with ExitStack() as stack:
        keep = stack.enter_context(tc.tile_pool(name="keep", bufs=1))
        raw_pool = stack.enter_context(tc.tile_pool(name="raw", bufs=RAW_BUFS))
        group_pool = stack.enter_context(tc.tile_pool(name="group", bufs=8))
        code_pool = stack.enter_context(tc.tile_pool(name="code", bufs=12))
        work = stack.enter_context(tc.tile_pool(name="work", bufs=2))
        psum = stack.enter_context(tc.psum_pool(name="psum", bufs=1))
        stack.enter_context(tc.manual_schedule())

        turn_banks = list(range(ACC_BANKS_HEAD, 8))
        turn_next = [0]

        def bank_tile(shape, dtype):
            index = turn_banks[turn_next[0] % len(turn_banks)]
            turn_next[0] += 1
            bank = psum.tile(shape, dtype, tag="bank%d" % index)
            return bank

        ident_f32 = keep.tile([P, P], F32)
        make_identity(nc, ident_f32[:])
        ident_bf16 = keep.tile([P, P], BF16)
        make_identity(nc, ident_bf16[:])
        bias_rows = keep.tile([P, P], BF16)
        nc.vector.memset(bias_rows[:], 0.0)
        nc.scalar.dma_start(out=bias_rows[0:ROW_BLOCKS, :], in_=b_ih.rearrange("(j p) -> j p", p=P))
        nc.scalar.dma_start(
            out=bias_rows[ROW_BLOCKS : ROW_BLOCKS + GATE_BLOCKS, :], in_=b_n.rearrange("(j p) -> j p", p=P)
        )
        table_in = keep.tile([P, 1], F32)
        table_out = keep.tile([P, 1], F32)
        nc.vector.memset(table_in[:], 0.0)
        nc.scalar.activation(out=table_out[:], in_=table_in[:], func=ACT.Sigmoid)

        block_order = [0, 1, 2, 3, 8, 9, 10, 11, 4, 5, 6, 7]

        items = [("whh", piece, 0) for piece in range(3)]
        head = block_order[:HEAD_BLOCKS]
        for c0 in range(0, QUARTERS, LPH):
            items += [("h", c, 0) for c in range(c0, c0 + LPH)]
            for j in head:
                items += [("w", j, c) for c in range(c0, c0 + LPH)]
        for j in block_order[HEAD_BLOCKS:]:
            items += [("w", j, c) for c in range(0, QUARTERS, SPAN)]

        def span(item):
            return 1 if item[1] in head else SPAN

        raw = {}
        prev_sb = keep.tile([P, 2 * HIDDEN], BF16)
        nc.sync.dma_start(
            out=prev_sb[:].rearrange("p (t k) -> p t k", t=2),
            in_=prev_rnn_hidden.rearrange("(t p) k -> p t k", p=P),
        )

        loads = []
        for kind, a, c in items:
            if kind == "whh":
                loads.append((kind, a, 0, 1))
            elif kind == "h" and a % LPH == 0:
                loads += [(kind, t, a, LPH) for t in range(2)]
            elif kind == "w" and a in head and c % LPH == 0:
                loads.append((kind, a, c, LPH))
            elif kind == "w" and a not in head and c % LPB == 0:
                loads.append((kind, a, c, LPB))
        raw_bufs = {1: RAW1_BUFS, LPB: RAWB_BUFS}
        in_use = {1: 0, LPB: 0}
        quarters_left = {}
        next_load = [0]

        def issue(load):
            kind, a, c, width = load
            piece = raw_pool.tile([P, width * QUARTER], BF16, tag="raw%d" % width, bufs=raw_bufs[width])
            if kind == "whh":
                nc.sync.dma_start(
                    out=piece[:].rearrange("p (j k) -> p j k", j=4),
                    in_=W_hh[4 * P * a : 4 * P * (a + 1), :].rearrange("(j p) k -> p j k", p=P),
                )
                raw[(kind, a, 0)] = [piece[:]]
            else:
                source = h if kind == "h" else W_ih
                nc.sync.dma_start(out=piece[:], in_=source[P * a : P * (a + 1), QUARTER * c : QUARTER * (c + width)])
                for i in range(width):
                    part = piece[:, QUARTER * i : QUARTER * (i + 1)]
                    if kind == "h":
                        raw.setdefault((kind, c + i, 0), []).append(part)
                    else:
                        raw[(kind, a, c + i)] = [part]
            quarters_left[load] = width

        def load_ahead():
            for index in range(next_load[0], len(loads)):
                width = loads[index][3]
                if in_use[width] >= raw_bufs[width]:
                    return
                issue(loads[index])
                in_use[width] += 1
                next_load[0] = index + 1

        def release(kind, a, c):
            for load in loads[: next_load[0]]:
                if load[0] == kind and load[1] == a and load[2] <= c < load[2] + load[3]:
                    quarters_left[load] -= 1
                    if quarters_left[load] == 0:
                        in_use[load[3]] -= 1

        load_ahead()

        banks_used = [0]

        def transpose_and_group(blocks, slabs):
            banks = len(blocks) // 4
            grouped = group_pool.tile([P, 2 * BANK_WORDS * banks], BF16, align_bytes=64, tag="grouped%d" % ((banks + 1) // 2))
            grouped_words = grouped[:].bitcast(F32)
            for b in range(banks):
                bank = bank_tile([P, BANK_WORDS], F32)
                for i in range(4):
                    nc.tensor.transpose(bank[:, P * i : P * (i + 1)], blocks[4 * b + i], ident_f32[:])
                src = bank[:].rearrange("p (s u c) -> p s c u", s=slabs, u=2)
                dst = grouped_words[:, BANK_WORDS * b : BANK_WORDS * (b + 1)].rearrange(
                    "p (s c u) -> p s c u", s=slabs, u=2
                )
                if banks_used[0] % VMOD == 1:
                    nc.vector.tensor_copy(out=dst, in_=src)
                else:
                    nc.scalar.copy(out=dst, in_=src)
                banks_used[0] += 1
            return grouped

        def quantise(grouped, codes, scales):
            nc.vector.quantize_mx(out=codes.bitcast(FP8X4), scales=scales, in_=grouped[:])

        def mx_pass(acc, w_codes, w_scales, x_codes, x_scales, start, stop):
            nc.tensor.matmul_mx(
                out=acc, lhsT=w_codes.bitcast(FP8X4), lhsT_scale=w_scales,
                rhs=x_codes.bitcast(FP8X4), rhs_scale=x_scales, start=start, stop=stop,
            )

        prev_words = prev_sb[:].bitcast(F32)
        prev_codes = keep.tile([P, BATCH], U32, align_bytes=64)
        prev_scales = keep.tile([P, BATCH], U8, align_bytes=64)
        prev_blocks = [prev_words[:, 256 * t + P * u : 256 * t + P * (u + 1)] for u in range(2) for t in range(2)]
        prev_grouped = transpose_and_group(prev_blocks, 1)
        prev_t_bank = bank_tile([P, 2 * BANK_WORDS], BF16)
        for f in range(GATE_BLOCKS):
            for t in range(2):
                nc.tensor.transpose(
                    prev_t_bank[:, BATCH * f + P * t : BATCH * f + P * (t + 1)],
                    prev_sb[:, HIDDEN * t + P * f : HIDDEN * t + P * (f + 1)],
                    ident_bf16[:],
                )
        prev_t = keep.tile([P, GATE_BLOCKS * BATCH], F32)
        nc.scalar.copy(out=prev_t[:], in_=prev_t_bank[:])
        bias_cols = keep.tile([P, ROW_BLOCKS + GATE_BLOCKS], F32)
        bias_neg = keep.tile([P, ROW_BLOCKS + GATE_BLOCKS], F32)

        def bias_transpose():
            bias_bank = bank_tile([P, 2 * BANK_WORDS], BF16)
            nc.tensor.transpose(bias_bank[:, 0:P], bias_rows[:], ident_bf16[:])
            nc.vector.tensor_copy(out=bias_cols[:], in_=bias_bank[:, 0 : ROW_BLOCKS + GATE_BLOCKS])
            nc.vector.tensor_scalar_mul(out=bias_neg[:], in0=bias_cols[:], scalar1=-1.0)

        whh_codes = keep.tile([P, ROW_BLOCKS * P], U32, align_bytes=64)
        whh_scales = keep.tile([P, ROW_BLOCKS * P], U8, align_bytes=64)
        h_codes = keep.tile([P, 16 * BATCH], U32, align_bytes=64)
        h_scales = keep.tile([P, 16 * BATCH], U8, align_bytes=64)
        w_codes = {}
        w_scales = {}
        groups = {}
        accs = {}

        def transposes(item):
            kind, a, c = item
            if kind == "h":
                words = [piece.bitcast(F32) for piece in raw[item]]
                groups[item] = []
                for half in range(2):
                    blocks = [
                        words[t][:, 256 * g + P * u : 256 * g + P * (u + 1)]
                        for g in (2 * half, 2 * half + 1)
                        for u in range(2)
                        for t in range(2)
                    ]
                    groups[item].append(transpose_and_group(blocks, 1))
            else:
                quarters = [c] if kind == "whh" else list(range(c, c + span(item)))
                words = [raw[(kind, a, q)][0].bitcast(F32) for q in quarters]
                groups[item] = [transpose_and_group([w[:, P * b : P * (b + 1)] for w in words for b in range(8)], 2)]

        def quantises(item):
            kind, a, c = item
            if kind == "whh":
                cols = slice(4 * P * a, 4 * P * (a + 1))
                quantise(groups[item][0], whh_codes[:, cols], whh_scales[:, cols])
            elif kind == "h":
                for half in range(2):
                    cols = slice(BATCH * (4 * a + 2 * half), BATCH * (4 * a + 2 * half + 2))
                    quantise(groups[item][half], h_codes[:, cols], h_scales[:, cols])
            else:
                codes = code_pool.tile([P, span(item) * QUARTER_PASSES * P], U32, align_bytes=64, tag="codes%d" % span(item))
                scales = code_pool.tile([P, span(item) * QUARTER_PASSES * P], U8, align_bytes=64, tag="scales%d" % span(item))
                quantise(groups[item][0], codes[:], scales[:])
                w_codes[item] = codes
                w_scales[item] = scales

        def hh_pass(acc, j, start, stop):
            cols = slice(P * j, P * (j + 1))
            mx_pass(acc, whh_codes[:, cols], whh_scales[:, cols], prev_codes[:], prev_scales[:], start, stop)

        hn_b = keep.tile([P, GATE_BLOCKS * BATCH], F32)
        reset_hn = keep.tile([P, GATE_BLOCKS * BATCH], F32)
        d_col = keep.tile([P, GATE_BLOCKS * BATCH], F32)
        prev_rows = prev_sb[:].rearrange("p (t k) -> p t k", t=2)

        def hn_products():
            for half in range(2):
                hn_bank = bank_tile([P, BANK_WORDS], F32)
                for i in range(2):
                    hh_pass(hn_bank[:, BATCH * i : BATCH * (i + 1)], 2 * GATE_BLOCKS + 2 * half + i, True, True)
                for i in range(2):
                    f = 2 * half + i
                    nc.scalar.activation(
                        out=hn_b[:, BATCH * f : BATCH * (f + 1)], in_=hn_bank[:, BATCH * i : BATCH * (i + 1)],
                        func=ACT.Identity, bias=bias_cols[:, ROW_BLOCKS + f : ROW_BLOCKS + f + 1],
                    )

        to_turn = []
        acc_count = [0]
        acc_tiles = {}

        def new_acc():
            k = acc_count[0]
            acc_count[0] += 1
            if k < HEAD_BLOCKS:
                per_bank = HEAD_BLOCKS // ACC_BANKS_HEAD
                index, half = divmod(k, per_bank)
                if half == 0:
                    acc_bank = psum.tile([P, BANK_WORDS], F32, tag="bank%d" % index)
                    acc_tiles[index] = acc_bank
                return acc_tiles[index][:, BATCH * half : BATCH * (half + 1)]
            if k == HEAD_BLOCKS:
                for index in range(ACC_BANKS_LATER, ACC_BANKS_HEAD):
                    turn_banks.append(index)
            index = (k - HEAD_BLOCKS) % ACC_BANKS_LATER
            acc_bank = psum.tile([P, BANK_WORDS], F32, tag="bank%d" % index)
            return acc_bank[:, 0:BATCH]

        def passes(item):
            kind, j, c = item
            sums_hh = j < 2 * GATE_BLOCKS
            if c == 0:
                accs[j] = new_acc()
                if sums_hh:
                    hh_pass(accs[j], j, True, False)
            for s in range(span(item) * QUARTER_PASSES):
                g = QUARTER_PASSES * c + s
                mx_pass(
                    accs[j], w_codes[item][:, P * s : P * (s + 1)], w_scales[item][:, P * s : P * (s + 1)],
                    h_codes[:, BATCH * g : BATCH * (g + 1)], h_scales[:, BATCH * g : BATCH * (g + 1)],
                    g == 0 and not sums_hh, g == 15,
                )
            if c + span(item) == QUARTERS:
                gate(j)

        def gate(j):
            kind, f = divmod(j, GATE_BLOCKS)
            cols = slice(BATCH * f, BATCH * (f + 1))
            if kind == 0:
                reset = work.tile([P, BATCH], F32, tag="reset")
                nc.scalar.activation(out=reset[:], in_=accs[j], func=ACT.Sigmoid, bias=bias_cols[:, j : j + 1])
                nc.vector.tensor_tensor(out=reset_hn[:, cols], in0=hn_b[:, cols], in1=reset[:], op=ALU.mult)
            elif kind == 2:
                pre = work.tile([P, BATCH], F32, tag="pre")
                nc.vector.tensor_tensor(out=pre[:], in0=accs[j], in1=reset_hn[:, cols], op=ALU.add)
                new = work.tile([P, BATCH], F32, tag="new")
                nc.scalar.activation(out=new[:], in_=pre[:], func=ACT.Tanh, bias=bias_cols[:, j : j + 1])
                nc.vector.tensor_tensor(out=d_col[:, cols], in0=prev_t[:, cols], in1=new[:], op=ALU.subtract)
            else:
                keepn = work.tile([P, BATCH], F32, tag="keepn")
                moved = work.tile([P, BATCH], F32, tag="moved")
                parts = 2 if j == block_order[-1] else 1
                width = BATCH // parts
                for i in range(parts):
                    part = slice(width * i, width * (i + 1))
                    nc.scalar.activation(
                        out=keepn[:, part], in_=accs[j][:, part], func=ACT.Sigmoid, bias=bias_neg[:, j : j + 1], scale=-1.0
                    )
                for i in range(parts):
                    part = slice(width * i, width * (i + 1))
                    nc.vector.tensor_tensor(
                        out=moved[:, part], in0=keepn[:, part], in1=d_col[:, BATCH * f + width * i : BATCH * f + width * (i + 1)], op=ALU.mult
                    )
                to_turn.append((j, moved))

        def turn_back():
            for j, turned in to_turn:
                kind, f = divmod(j, GATE_BLOCKS)
                cols = slice(BATCH * f, BATCH * (f + 1))
                back = bank_tile([P, BANK_WORDS], F32)
                for t in range(2):
                    nc.tensor.transpose(back[:, P * t : P * (t + 1)], turned[:, P * t : P * (t + 1)], ident_f32[:])
                out_sb = work.tile([P, BATCH], F32, tag="out_sb")
                if j == block_order[-1]:
                    for t in range(2):
                        nc.vector.tensor_tensor(
                            out=out_sb[:, P * t : P * (t + 1)], in0=prev_sb[:, HIDDEN * t + P * f : HIDDEN * t + P * (f + 1)],
                            in1=back[:, P * t : P * (t + 1)], op=ALU.subtract,
                        )
                        nc.sync.dma_start(out=out[P * t : P * (t + 1), P * f : P * (f + 1)], in_=out_sb[:, P * t : P * (t + 1)])
                else:
                    prev_f = prev_rows[:, :, P * f : P * (f + 1)]
                    nc.vector.tensor_tensor(
                        out=out_sb[:].rearrange("p (t r) -> p t r", t=2), in0=prev_f,
                        in1=back[:, 0:BATCH].rearrange("p (t r) -> p t r", t=2), op=ALU.subtract,
                    )
                    nc.sync.dma_start(
                        out=out.rearrange("(t p) r -> p t r", p=P)[:, :, P * f : P * (f + 1)],
                        in_=out_sb[:].rearrange("p (t r) -> p t r", t=2),
                    )
            to_turn.clear()

        units = [items[0:3]] + [u for c in range(QUARTERS) for u in (items[3 + 3 * c : 4 + 3 * c], items[4 + 3 * c : 6 + 3 * c])] + [items[k : k + 4] for k in range(15, len(items), 4)]
        quantise(prev_grouped, prev_codes[:], prev_scales[:])
        done_items = [0]
        for i in range(len(units) + LAG):
            if i < len(units):
                for k, item in enumerate(units[i]):
                    transposes(item)
                    if item[0] == "h":
                        release("h", 0, item[1])
                        release("h", 1, item[1])
                    else:
                        for q in range(item[2], item[2] + (1 if item[0] == "whh" else span(item))):
                            release(item[0], item[1], q)
                    load_ahead()
                    if k >= QLAG:
                        quantises(units[i][k - QLAG])
                if i == 0:
                    bias_transpose()
                turn_back()
                for item in units[i][max(0, len(units[i]) - QLAG) :]:
                    quantises(item)
            if i >= LAG:
                for item in units[i - LAG]:
                    if item == ("whh", 2, 0):
                        hn_products()
                    if item[0] == "w":
                        passes(item)
        turn_back()
